import numpy as np
import ml_dtypes


def mxq(x, axis, fmt="e4m3"):
    dtype, down = {"e4m3": (ml_dtypes.float8_e4m3fn, 7), "e5m2": (ml_dtypes.float8_e5m2, 14)}[fmt]
    v = np.moveaxis(np.asarray(x, np.float32).astype(ml_dtypes.bfloat16).astype(np.float64), axis, -1)
    blocks = v.reshape(v.shape[:-1] + (-1, 32))
    amax = np.abs(blocks).max(-1, keepdims=True)
    byte = np.maximum(np.where(amax > 0, np.frexp(amax)[1] - 1 + 127, 0) - down, 1)
    scale = np.exp2(byte - 127.0)
    codes = (blocks / scale).astype(np.float32).astype(dtype).astype(np.float64)
    return np.moveaxis((codes * scale).reshape(v.shape), -1, axis)


WIDE = False


def mx_kscale(k):
    if not WIDE:
        return np.ones(k)
    levels = np.array([10, -10, 5, -5, 0])
    a = np.random.permutation(np.resize(levels, k // 512 * 4)).reshape(k // 512, 4)
    idx = np.arange(k)
    return np.exp2(a[idx // 512, idx % 128 // 32])


BF16 = ml_dtypes.bfloat16


def bf(x):
    return np.asarray(x, np.float32).astype(BF16)


def f64(x):
    return np.asarray(x).astype(np.float64)


E2M1 = np.array([0.0, 0.5, 1.0, 1.5, 2.0, 3.0, 4.0, 6.0, -0.0, -0.5, -1.0, -1.5, -2.0, -3.0, -4.0, -6.0])


def pack_weight(w, fmt):
    k, n = w.shape
    w = f64(bf(w)).reshape(k // 32, 32, n)
    amax = np.abs(w).max(1)
    if fmt == "e4m3":
        byte = np.frexp(amax)[1] - 1 + 127 - 7
    else:
        mant, ex = np.frexp(amax / 6.0)
        byte = np.where(mant > 0.5, ex, ex - 1) + 127
    byte = np.clip(np.where(amax > 0, byte, 1), 1, 254)
    scaled = (w * np.exp2(127.0 - byte)[:, None, :]).reshape(k, n).astype(np.float32)
    by_word = np.ascontiguousarray(scaled.reshape(k // 512, 128, 4, n).transpose(0, 1, 3, 2))
    if fmt == "e4m3":
        words = by_word.astype(ml_dtypes.float8_e4m3fn).view(np.uint8)
    else:
        c = by_word.astype(ml_dtypes.float4_e2m1fn).view(np.uint8) & 0xF
        words = c[..., 0::2] | (c[..., 1::2] << 4)
    return np.ascontiguousarray(words), np.ascontiguousarray(byte.astype(np.uint8).reshape(k // 512, 16, n))


def unpack_weight(words, scales, fmt):
    g, p, n, _ = words.shape
    if fmt == "e4m3":
        vals = np.ascontiguousarray(words).view(ml_dtypes.float8_e4m3fn).astype(np.float64)
    else:
        nib = np.empty((g, p, n, 4), np.uint8)
        nib[..., 0::2] = words & 0xF
        nib[..., 1::2] = words >> 4
        vals = E2M1[nib]
    vals = vals * np.repeat(np.exp2(scales.astype(np.float64) - 127.0), 8, axis=1)[..., None]
    return vals.transpose(0, 1, 3, 2).reshape(g * 512, n)


B, N, HD, ED, F = 1, 64, 384, 256, 512
TD = HD + HD
MD = TD + ED
EPS = 1e-5
FMT = "e4m3"


def layer_norm(x, g, b):
    mu = x.mean(-1, keepdims=True)
    var = x.var(-1, keepdims=True)
    return (x - mu) * (1.0 / np.sqrt(var + EPS)) * g + b


def setup_inputs():
    t = mx_kscale(F)
    rx = mx_kscale(MD)[:HD]
    r = np.concatenate([rx, rx, np.ones(ED)])
    hid = bf(np.maximum(np.random.standard_normal((B, N, N, F)), 0.0) * t)
    x_down = bf(np.random.standard_normal((B, N, HD)) * rx)
    p_ln = bf(np.random.standard_normal((B, N, N, ED)))
    W2_words, W2_scales = pack_weight(np.random.standard_normal((F, MD)) / np.sqrt(F) / t[:, None] * r, FMT)
    b2 = bf(0.1 * np.random.standard_normal(MD) * r)
    Wo_words, Wo_scales = pack_weight(np.random.standard_normal((MD, ED)) / np.sqrt(MD) / r[:, None], FMT)
    bo = bf(0.1 * np.random.standard_normal(ED))
    ln_out_g = bf(1.0 + 0.1 * np.random.standard_normal(ED))
    ln_out_b = bf(0.1 * np.random.standard_normal(ED))
    return {"hid": hid,
            "x_down": x_down,
            "p_ln": p_ln,
            "W2_words": W2_words,
            "W2_scales": W2_scales,
            "b2": b2,
            "Wo_words": Wo_words,
            "Wo_scales": Wo_scales,
            "bo": bo,
            "ln_out_g": ln_out_g,
            "ln_out_b": ln_out_b}


def reference(hid, x_down, p_ln, W2_words, W2_scales, b2, Wo_words, Wo_scales, bo, ln_out_g, ln_out_b):
    xd, pl = f64(x_down), f64(p_ln)
    edge_bias = np.concatenate([np.broadcast_to(xd[:, :, None, :], (B, N, N, HD)),
                                np.broadcast_to(xd[:, None, :, :], (B, N, N, HD))], axis=-1)
    z_in = np.concatenate([edge_bias, pl], axis=-1)
    m = np.maximum((mxq(f64(hid), 3, "e4m3") @ unpack_weight(W2_words, W2_scales, FMT)) + f64(b2), 0.0)
    z = (mxq(m + z_in, 3, "e4m3") @ unpack_weight(Wo_words, Wo_scales, FMT)) + f64(bo)
    return pl + layer_norm(z, f64(ln_out_g), f64(ln_out_b))

@@ -1,0 +1,373 @@
+import concourse.mybir as mybir
+from concourse.masks import make_identity
+
+F32 = mybir.dt.float32
+BF16 = mybir.dt.bfloat16
+I32 = mybir.dt.int32
+U32 = mybir.dt.uint32
+U8 = mybir.dt.uint8
+FP8X4 = mybir.dt.float8_e4m3fn_x4
+ALU = mybir.AluOpType
+ACT = mybir.ActivationFunctionType
+
+P = 128
+PACK = 4
+K_PASS = P * PACK
+N_MAX = 512
+NODES = 64
+HD = 384
+ED = 256
+F = 512
+MD = HD + HD + ED
+PASSES = MD // K_PASS
+SLABS = MD // P
+SLABS_PER_PASS = SLABS // PASSES
+X_SLABS = HD // P
+P_SLABS = ED // P
+WORD_ROWS = P // PACK
+ROWS = NODES * NODES
+BLOCK = 1024
+BLOCKS = ROWS // BLOCK
+HALVES = BLOCK // N_MAX
+TILES = BLOCK // P
+ALL_TILES = ROWS // P
+PAIRS_PER_BLOCK = TILES // 2
+ALL_PAIRS = ALL_TILES // 2
+SLABS_PER_STEP = SLABS // TILES
+LAG = 3
+SLAB_LEAD = TILES + LAG + 1
+PAIR_LEAD = SLAB_LEAD + TILES + LAG
+LOAD_LEAD = PAIR_LEAD + TILES
+I_PER_HALF = N_MAX // NODES
+EPS = 1e-5
+
+FLOPS = 2 * ROWS * F * MD + 2 * ROWS * MD * ED
+
+
+def tile_edgeupdaterwrapper_v01_pb_t_kernel(
+    tc, hid, x_down, p_ln, W2_words, W2_scales, b2, Wo_words, Wo_scales, bo, ln_out_g, ln_out_b, out
+):
+    nc = tc.nc
+    hid_rows_all = hid.rearrange("b i j k -> (b i j) k")
+    p_rows_all = p_ln.rearrange("b i j d -> (b i j) d")
+    out_rows_all = out.rearrange("b i j d -> (b i j) d")
+
+    with tc.tile_pool(name="consts", bufs=1) as consts, tc.tile_pool(name="blocks", bufs=2) as blocks, tc.tile_pool(
+        name="work", bufs=3
+    ) as work, tc.tile_pool(name="stats", bufs=4) as stats, tc.psum_pool(name="psum", bufs=2) as psum:
+        w2_scales = consts.tile([P, MD], U8, align_bytes=64)
+        wo_scales = consts.tile([P, PASSES, ED], U8, align_bytes=64)
+        nc.vector.memset(w2_scales[:].bitcast(I32), 0)
+        nc.vector.memset(wo_scales[:].rearrange("p g n -> p (g n)").bitcast(I32), 0)
+        for quad in range(4):
+            nc.sync.dma_start(
+                out=w2_scales[32 * quad : 32 * quad + 4, :].bitcast(I32),
+                in_=W2_scales[0, 4 * quad : 4 * quad + 4, :].bitcast(I32),
+            )
+        w2_words = consts.tile([P, MD], U32, align_bytes=64)
+        nc.sync.dma_start(
+            out=w2_words[:].bitcast(I32), in_=W2_words.rearrange("g p n t -> (g p) (n t)").bitcast(I32)
+        )
+        for quad in range(4):
+            nc.sync.dma_start(
+                out=wo_scales[32 * quad : 32 * quad + 4, :, :].bitcast(I32),
+                in_=Wo_scales[:, 4 * quad : 4 * quad + 4, :].rearrange("g r n -> r g n").bitcast(I32),
+            )
+        wo_words = consts.tile([P, PASSES, ED], U32, align_bytes=64)
+        nc.sync.dma_start(
+            out=wo_words[:].bitcast(I32), in_=Wo_words.rearrange("g p n t -> p g (n t)").bitcast(I32)
+        )
+
+        ident_f32 = consts.tile([P, P], F32)
+        make_identity(nc, ident_f32[:])
+        ident_bf16 = consts.tile([P, P], BF16)
+        make_identity(nc, ident_bf16[:])
+        eps_col = consts.tile([P, 1], F32)
+        nc.vector.memset(eps_col[:], EPS)
+
+        bo_rows = consts.tile([P, ED], BF16)
+        nc.scalar.dma_start(out=bo_rows[:], in_=bo.partition_broadcast(P))
+        gain_rows = consts.tile([P, ED], BF16)
+        nc.scalar.dma_start(out=gain_rows[:], in_=ln_out_g.partition_broadcast(P))
+        beta_rows = consts.tile([P, ED], BF16)
+        nc.scalar.dma_start(out=beta_rows[:], in_=ln_out_b.partition_broadcast(P))
+
+        b2_stage = consts.tile([P, P], BF16)
+        nc.vector.memset(b2_stage[:], 0.0)
+        nc.scalar.dma_start(out=b2_stage[0:SLABS, :], in_=b2.rearrange("(c f) -> c f", f=P))
+        b2_t = psum.tile([P, P], BF16, tag="from_rows", bufs=1)
+        nc.tensor.transpose(b2_t[:], b2_stage[:], ident_bf16[:])
+        b2_cols = consts.tile([P, SLABS], F32)
+        nc.vector.tensor_copy(out=b2_cols[:], in_=b2_t[:, 0:SLABS])
+        neg_b2_cols = consts.tile([P, SLABS], F32)
+        nc.vector.tensor_scalar(
+            out=neg_b2_cols[:], in0=b2_t[:, 0:SLABS], scalar1=-1.0, scalar2=None, op0=ALU.mult
+        )
+
+        x_stage = consts.tile([P, HD], BF16)
+        nc.vector.memset(x_stage[NODES:P, :], 0.0)
+        nc.scalar.dma_start(out=x_stage[0:NODES, :], in_=x_down.rearrange("b n d -> (b n) d"))
+        x_t = psum.tile([P, X_SLABS, P], BF16, tag="from_rows", bufs=1)
+        for c in range(X_SLABS):
+            nc.tensor.transpose(x_t[:, c, :], x_stage[:, P * c : P * (c + 1)], ident_bf16[:])
+        b2_plus_xi = consts.tile([P, X_SLABS, NODES], F32)
+        b2_plus_xj = consts.tile([P, X_SLABS, NODES], F32)
+        for c in range(X_SLABS):
+            nc.scalar.activation(
+                out=b2_plus_xi[:, c, :], in_=x_t[:, c, 0:NODES], func=ACT.Identity, bias=b2_cols[:, c : c + 1]
+            )
+            nc.scalar.activation(
+                out=b2_plus_xj[:, c, :],
+                in_=x_t[:, c, 0:NODES],
+                func=ACT.Identity,
+                bias=b2_cols[:, X_SLABS + c : X_SLABS + c + 1],
+            )
+
+
+        p_all = consts.tile([P, ALL_TILES, ED], BF16)
+        residual_all = consts.tile([P, ALL_TILES, ED], F32)
+
+        hid_of = {}
+        operand_of = {}
+        grouped_of = {}
+        product_of = {}
+        planes_of = {}
+        y_of = {}
+        s_grouped_of = {}
+        s_codes_of = {}
+        z_of = {}
+        normed_of = {}
+        result_of = {}
+
+        def load_block(b):
+            rows = slice(BLOCK * b, BLOCK * (b + 1))
+            hid_rows = blocks.tile([P, TILES, F], BF16)
+            nc.sync.dma_start(out=hid_rows[:], in_=hid_rows_all[rows, :].rearrange("(n q) k -> q n k", q=P))
+            nc.sync.dma_start(
+                out=p_all[:, TILES * b : TILES * (b + 1), :],
+                in_=p_rows_all[rows, :].rearrange("(n q) d -> q n d", q=P),
+            )
+            hid_of[b] = hid_rows
+            nc.gpsimd.tensor_tensor(
+                out=residual_all[:, TILES * b : TILES * (b + 1), :],
+                in0=p_all[:, TILES * b : TILES * (b + 1), :],
+                in1=beta_rows[:].unsqueeze(1).to_broadcast([P, TILES, ED]),
+                op=ALU.add,
+            )
+
+        def transpose_pair(pair):
+            b, local = divmod(pair, PAIRS_PER_BLOCK)
+            if local == 0:
+                hid_codes = blocks.tile([P, BLOCK], U32, align_bytes=64, bufs=3)
+                hid_scales = blocks.tile([P, BLOCK], U8, align_bytes=64, bufs=3)
+                b2_plus_p = blocks.tile([P, P_SLABS, BLOCK], F32, bufs=3)
+                operand_of[b] = (hid_codes, hid_scales, b2_plus_p)
+            word_t = psum.tile([P, 2, 2, P], F32, tag="word_t", bufs=1)
+            for m in range(2):
+                words = hid_of[b][:, 2 * local + m, :].bitcast(F32)
+                for u in range(2):
+                    nc.tensor.transpose(word_t[:, m, u, :], words[:, u : F // 2 : 2], ident_f32[:])
+            p_t = psum.tile([P, P_SLABS, 2 * P], BF16, tag="from_rows", bufs=1)
+            for m in range(2):
+                for c in range(P_SLABS):
+                    nc.tensor.transpose(
+                        p_t[:, c, P * m : P * (m + 1)], p_all[:, 2 * pair + m, P * c : P * (c + 1)], ident_bf16[:]
+                    )
+            hid_grouped = work.tile([P, 2, P, PACK], BF16, align_bytes=64, bufs=4)
+            nc.scalar.copy(
+                out=hid_grouped[:]
+                .rearrange("p n q t -> p (n q t)")
+                .bitcast(F32)
+                .rearrange("p (n q u) -> p n q u", n=2, u=2),
+                in_=word_t[:].rearrange("p n u q -> p n q u"),
+            )
+            grouped_of[pair] = hid_grouped
+            for c in range(P_SLABS):
+                nc.scalar.activation(
+                    out=operand_of[b][2][:, c, 2 * P * local : 2 * P * (local + 1)],
+                    in_=p_t[:, c, :],
+                    func=ACT.Identity,
+                    bias=b2_cols[:, 2 * X_SLABS + c : 2 * X_SLABS + c + 1],
+                )
+
+        def quantise_hid_pair(pair):
+            b, local = divmod(pair, PAIRS_PER_BLOCK)
+            cols = slice(2 * P * local, 2 * P * (local + 1))
+            nc.vector.quantize_mx(
+                out=operand_of[b][0][:, cols].bitcast(FP8X4),
+                scales=operand_of[b][1][:, cols],
+                in_=grouped_of[pair][:].rearrange("p n q t -> p (n q t)"),
+            )
+
+        def first_matmul(b, c):
+            hid_codes, hid_scales = operand_of[b][0:2]
+            for h in range(HALVES):
+                cols = slice(N_MAX * h, N_MAX * (h + 1))
+                product = psum.tile([P, N_MAX], F32, tag="product", bufs=4)
+                nc.tensor.matmul_mx(
+                    out=product[:],
+                    lhsT=w2_words[:, P * c : P * (c + 1)].bitcast(FP8X4),
+                    lhsT_scale=w2_scales[:, P * c : P * (c + 1)],
+                    rhs=hid_codes[:, cols].bitcast(FP8X4),
+                    rhs_scale=hid_scales[:, cols],
+                    start=True,
+                    stop=True,
+                )
+                product_of[(b, c, h)] = product
+
+        def make_s(b, c):
+            b2_plus_p = operand_of[b][2]
+            if c == 0:
+                s_planes = blocks.tile([P, PASSES, PACK, BLOCK], BF16, bufs=3)
+                planes_of[b] = s_planes
+            s_slab = work.tile([P, BLOCK], BF16, bufs=4)
+            for h in range(HALVES):
+                cols = slice(N_MAX * h, N_MAX * (h + 1))
+                first_i = (BLOCK * b + N_MAX * h) // NODES
+                if c < X_SLABS:
+                    b2_plus_z = (
+                        b2_plus_xi[:, c, first_i : first_i + I_PER_HALF]
+                        .unsqueeze(2)
+                        .to_broadcast([P, I_PER_HALF, NODES])
+                    )
+                elif c < 2 * X_SLABS:
+                    b2_plus_z = b2_plus_xj[:, c - X_SLABS, :].unsqueeze(1).to_broadcast([P, I_PER_HALF, NODES])
+                else:
+                    b2_plus_z = b2_plus_p[:, c - 2 * X_SLABS, cols].rearrange("f (i j) -> f i j", j=NODES)
+                nc.vector.scalar_tensor_tensor(
+                    out=s_slab[:, cols].rearrange("f (i j) -> f i j", j=NODES),
+                    in0=product_of[(b, c, h)][:].rearrange("f (i j) -> f i j", j=NODES),
+                    scalar=neg_b2_cols[:, c : c + 1],
+                    in1=b2_plus_z,
+                    op0=ALU.max,
+                    op1=ALU.add,
+                )
+            first_p = WORD_ROWS * (c % SLABS_PER_PASS)
+            for t in range(PACK):
+                nc.sync.dma_start(
+                    out=planes_of[b][first_p : first_p + WORD_ROWS, c // SLABS_PER_PASS, t, :],
+                    in_=s_slab[t:P:PACK, :],
+                )
+
+        def group_tile(tile, copy):
+            b, n = divmod(tile, TILES)
+            s_grouped = work.tile([P, PASSES, P, PACK], BF16, align_bytes=64, bufs=6)
+            for g in range(PASSES):
+                copy(
+                    out=s_grouped[:, g].rearrange("p (c i) t -> p c t i", i=4),
+                    in_=planes_of[b][:, g, :, P * n : P * (n + 1)].rearrange("p t (c i) -> p c t i", i=4),
+                )
+            s_grouped_of[tile] = s_grouped
+
+        def quantise_s(tile):
+            s_codes = work.tile([P, PASSES, P], U32, align_bytes=64)
+            s_scales = work.tile([P, PASSES, P], U8, align_bytes=64)
+            nc.vector.quantize_mx(
+                out=s_codes[:].rearrange("p g q -> p (g q)").bitcast(FP8X4),
+                scales=s_scales[:].rearrange("p g q -> p (g q)"),
+                in_=s_grouped_of[tile][:].rearrange("p g q t -> p (g q t)"),
+            )
+            s_codes_of[tile] = (s_codes, s_scales)
+
+        def second_matmul(tile):
+            s_codes, s_scales = s_codes_of[tile]
+            y = psum.tile([P, ED], F32, tag="y", bufs=2)
+            for g in range(PASSES):
+                nc.tensor.matmul_mx(
+                    out=y[:],
+                    lhsT=s_codes[:, g, :].bitcast(FP8X4),
+                    lhsT_scale=s_scales[:, g, :],
+                    rhs=wo_words[:, g, :].bitcast(FP8X4),
+                    rhs_scale=wo_scales[:, g, :],
+                    start=(g == 0),
+                    stop=(g == PASSES - 1),
+                )
+            y_of[tile] = y
+
+        def add_bo(tile):
+            z = work.tile([P, ED], F32, bufs=4)
+            z_sum = stats.tile([P, 1], F32)
+            nc.vector.scalar_tensor_tensor(
+                out=z[:], in0=y_of[tile][:], scalar=0.0, in1=bo_rows[:], op0=ALU.add, op1=ALU.add, accum_out=z_sum[:]
+            )
+            z_of[tile] = (z, z_sum)
+
+        def normalise(tile):
+            z, z_sum = z_of[tile]
+            if tile % 2 == 0:
+                normed = work.tile([P, 2, ED], F32)
+                normed_of[tile // 2] = normed
+            neg_mean = stats.tile([P, 1], F32)
+            nc.scalar.mul(out=neg_mean[:], in_=z_sum[:], mul=-1.0 / ED)
+            unused = work.tile([P, ED], F32, bufs=2)
+            sq_sum = stats.tile([P, 1], F32)
+            nc.scalar.activation(
+                out=unused[:], in_=z[:], func=ACT.Square, bias=neg_mean[:], accum_out=sq_sum[:]
+            )
+            rstd = stats.tile([P, 1], F32)
+            nc.scalar.activation(
+                out=rstd[:], in_=sq_sum[:], func=ACT.Abs_reciprocal_sqrt, scale=1.0 / ED, bias=eps_col[:]
+            )
+            shift = stats.tile([P, 1], F32)
+            nc.scalar.activation(out=shift[:], in_=neg_mean[:], func=ACT.Copy, scale=rstd[:])
+            nc.scalar.activation(
+                out=normed_of[tile // 2][:, tile % 2, :], in_=z[:], func=ACT.Identity, scale=rstd[:], bias=shift[:]
+            )
+
+        def finish_pair(pair):
+            scaled = work.tile([P, 2, ED], F32)
+            nc.gpsimd.tensor_tensor(
+                out=scaled[:],
+                in0=normed_of[pair][:],
+                in1=gain_rows[:].unsqueeze(1).to_broadcast([P, 2, ED]),
+                op=ALU.mult,
+            )
+            result = work.tile([P, 2, ED], F32, bufs=4)
+            nc.gpsimd.tensor_tensor(
+                out=result[:], in0=scaled[:], in1=residual_all[:, 2 * pair : 2 * pair + 2, :], op=ALU.add
+            )
+            result_of[pair] = result
+
+        def store_pair(pair):
+            nc.sync.dma_start(
+                out=out_rows_all[2 * P * pair : 2 * P * (pair + 1), :].rearrange("(n q) d -> q n d", q=P),
+                in_=result_of[pair][:],
+            )
+
+        def grouped_by_scalar(tile):
+            return tile % 2 == 1 and tile + SLAB_LEAD < ALL_TILES
+
+        load_block(0)
+        load_block(1)
+        with tc.manual_schedule():
+            for step in range(-PAIR_LEAD, ALL_TILES + 2 + LAG + 1):
+                if (step + LOAD_LEAD) % TILES == 0 and 2 <= (step + LOAD_LEAD) // TILES < BLOCKS:
+                    load_block((step + LOAD_LEAD) // TILES)
+                if (step + PAIR_LEAD - LAG) % 2 == 0 and 0 <= (step + PAIR_LEAD - LAG) // 2 < ALL_PAIRS:
+                    quantise_hid_pair((step + PAIR_LEAD - LAG) // 2)
+                if 0 <= step < ALL_TILES:
+                    if not grouped_by_scalar(step):
+                        group_tile(step, nc.vector.tensor_copy)
+                    quantise_s(step)
+                if 0 <= step + SLAB_LEAD + 1 < ALL_TILES:
+                    b, k = divmod(step + SLAB_LEAD + 1, TILES)
+                    for c in range(SLABS_PER_STEP * k, SLABS_PER_STEP * (k + 1)):
+                        first_matmul(b, c)
+                if 0 <= step < ALL_TILES:
+                    second_matmul(step)
+                if 0 <= step - 1 < ALL_TILES:
+                    add_bo(step - 1)
+                if 0 <= step + SLAB_LEAD < ALL_TILES:
+                    b, k = divmod(step + SLAB_LEAD, TILES)
+                    for c in range(SLABS_PER_STEP * k, SLABS_PER_STEP * (k + 1)):
+                        make_s(b, c)
+                if 0 <= step - 1 < ALL_TILES:
+                    normalise(step - 1)
+                if 0 <= step + LAG < ALL_TILES and grouped_by_scalar(step + LAG):
+                    group_tile(step + LAG, nc.scalar.copy)
+                if (step + PAIR_LEAD) % 2 == 0 and 0 <= (step + PAIR_LEAD) // 2 < ALL_PAIRS:
+                    transpose_pair((step + PAIR_LEAD) // 2)
+                if step % 2 == 0 and 0 <= step // 2 - 1 < ALL_PAIRS:
+                    finish_pair(step // 2 - 1)
+                if (step - LAG) % 2 == 0 and 0 <= (step - LAG) // 2 - 1 < ALL_PAIRS:
+                    store_pair((step - LAG) // 2 - 1)

@@ -136,7 +136,8 @@ def tile_edgeupdaterwrapper_v01_pb_t_kernel(
         s_grouped_of = {}
         s_codes_of = {}
         z_of = {}
-        normed_of = {}
+        stats_of = {}
+        centred_of = {}
         result_of = {}
 
         def load_block(b):
@@ -285,48 +286,52 @@ def tile_edgeupdaterwrapper_v01_pb_t_kernel(
             y_of[tile] = y
 
         def add_bo(tile):
-            z = work.tile([P, ED], F32, bufs=4)
+            z = work.tile([P, ED], F32, bufs=6)
             z_sum = stats.tile([P, 1], F32)
             nc.vector.scalar_tensor_tensor(
                 out=z[:], in0=y_of[tile][:], scalar=0.0, in1=bo_rows[:], op0=ALU.add, op1=ALU.add, accum_out=z_sum[:]
             )
             z_of[tile] = (z, z_sum)
 
-        def normalise(tile):
+        def row_statistics(tile):
             z, z_sum = z_of[tile]
-            if tile % 2 == 0:
-                normed = work.tile([P, 2, ED], F32)
-                normed_of[tile // 2] = normed
-            neg_mean = stats.tile([P, 1], F32)
+            neg_mean = stats.tile([P, 1], F32, bufs=8)
             nc.scalar.mul(out=neg_mean[:], in_=z_sum[:], mul=-1.0 / ED)
             unused = work.tile([P, ED], F32, bufs=2)
             sq_sum = stats.tile([P, 1], F32)
             nc.scalar.activation(
                 out=unused[:], in_=z[:], func=ACT.Square, bias=neg_mean[:], accum_out=sq_sum[:]
             )
-            rstd = stats.tile([P, 1], F32)
+            rstd = stats.tile([P, 1], F32, bufs=8)
             nc.scalar.activation(
                 out=rstd[:], in_=sq_sum[:], func=ACT.Abs_reciprocal_sqrt, scale=1.0 / ED, bias=eps_col[:]
             )
-            shift = stats.tile([P, 1], F32)
-            nc.scalar.activation(out=shift[:], in_=neg_mean[:], func=ACT.Copy, scale=rstd[:])
-            nc.scalar.activation(
-                out=normed_of[tile // 2][:, tile % 2, :], in_=z[:], func=ACT.Identity, scale=rstd[:], bias=shift[:]
-            )
+            stats_of[tile] = (neg_mean, rstd)
 
-        def finish_pair(pair):
-            scaled = work.tile([P, 2, ED], F32)
-            nc.gpsimd.tensor_tensor(
-                out=scaled[:],
-                in0=normed_of[pair][:],
-                in1=gain_rows[:].unsqueeze(1).to_broadcast([P, 2, ED]),
-                op=ALU.mult,
+        def apply_gain(tile):
+            centred = work.tile([P, ED], F32)
+            nc.vector.scalar_tensor_tensor(
+                out=centred[:],
+                in0=z_of[tile][0][:],
+                scalar=stats_of[tile][0][:],
+                in1=gain_rows[:],
+                op0=ALU.add,
+                op1=ALU.mult,
             )
-            result = work.tile([P, 2, ED], F32, bufs=4)
-            nc.gpsimd.tensor_tensor(
-                out=result[:], in0=scaled[:], in1=residual_all[:, 2 * pair : 2 * pair + 2, :], op=ALU.add
+            centred_of[tile] = centred
+
+        def add_residual(tile):
+            if tile % 2 == 0:
+                result = work.tile([P, 2, ED], F32, bufs=4)
+                result_of[tile // 2] = result
+            nc.vector.scalar_tensor_tensor(
+                out=result_of[tile // 2][:, tile % 2, :],
+                in0=centred_of[tile][:],
+                scalar=stats_of[tile][1][:],
+                in1=residual_all[:, tile, :],
+                op0=ALU.mult,
+                op1=ALU.add,
             )
-            result_of[pair] = result
 
         def store_pair(pair):
             nc.sync.dma_start(
@@ -335,19 +340,22 @@ def tile_edgeupdaterwrapper_v01_pb_t_kernel(
             )
 
         def grouped_by_scalar(tile):
-            return tile % 2 == 1 and tile + SLAB_LEAD < ALL_TILES
+            return tile + SLAB_LEAD < ALL_TILES
 
         load_block(0)
         load_block(1)
         with tc.manual_schedule():
             for step in range(-PAIR_LEAD, ALL_TILES + 2 + LAG + 1):
+                done = step - 1 - LAG
                 if (step + LOAD_LEAD) % TILES == 0 and 2 <= (step + LOAD_LEAD) // TILES < BLOCKS:
                     load_block((step + LOAD_LEAD) // TILES)
                 if (step + PAIR_LEAD - LAG) % 2 == 0 and 0 <= (step + PAIR_LEAD - LAG) // 2 < ALL_PAIRS:
                     quantise_hid_pair((step + PAIR_LEAD - LAG) // 2)
+                if 0 <= step < ALL_TILES and not grouped_by_scalar(step):
+                    group_tile(step, nc.vector.tensor_copy)
+                if 0 <= done < ALL_TILES:
+                    apply_gain(done)
                 if 0 <= step < ALL_TILES:
-                    if not grouped_by_scalar(step):
-                        group_tile(step, nc.vector.tensor_copy)
                     quantise_s(step)
                 if 0 <= step + SLAB_LEAD + 1 < ALL_TILES:
                     b, k = divmod(step + SLAB_LEAD + 1, TILES)
@@ -361,13 +369,13 @@ def tile_edgeupdaterwrapper_v01_pb_t_kernel(
                     b, k = divmod(step + SLAB_LEAD, TILES)
                     for c in range(SLABS_PER_STEP * k, SLABS_PER_STEP * (k + 1)):
                         make_s(b, c)
+                if 0 <= done < ALL_TILES:
+                    add_residual(done)
+                    if done % 2 == 1:
+                        store_pair(done // 2)
                 if 0 <= step - 1 < ALL_TILES:
-                    normalise(step - 1)
+                    row_statistics(step - 1)
                 if 0 <= step + LAG < ALL_TILES and grouped_by_scalar(step + LAG):
                     group_tile(step + LAG, nc.scalar.copy)
                 if (step + PAIR_LEAD) % 2 == 0 and 0 <= (step + PAIR_LEAD) // 2 < ALL_PAIRS:
                     transpose_pair((step + PAIR_LEAD) // 2)
-                if step % 2 == 0 and 0 <= step // 2 - 1 < ALL_PAIRS:
-                    finish_pair(step // 2 - 1)
-                if (step - LAG) % 2 == 0 and 0 <= (step - LAG) // 2 - 1 < ALL_PAIRS:
-                    store_pair((step - LAG) // 2 - 1)

@@ -33,9 +33,9 @@ TILES = BLOCK // P
 ALL_TILES = ROWS // P
 PAIRS_PER_BLOCK = TILES // 2
 ALL_PAIRS = ALL_TILES // 2
-SLABS_PER_STEP = SLABS // TILES
+assert SLABS == TILES
 LAG = 3
-SLAB_LEAD = TILES + LAG + 1
+SLAB_LEAD = TILES + LAG + 2
 PAIR_LEAD = SLAB_LEAD + TILES + LAG
 LOAD_LEAD = PAIR_LEAD + TILES
 I_PER_HALF = N_MAX // NODES
@@ -136,8 +136,11 @@ def tile_edgeupdaterwrapper_v01_pb_t_kernel(
         s_grouped_of = {}
         s_codes_of = {}
         z_of = {}
-        stats_of = {}
-        centred_of = {}
+        slab_of = {}
+        sums_of = {}
+        mean_var_of = {}
+        rstd_of = {}
+        normed_of = {}
         result_of = {}
 
         def load_block(b):
@@ -174,15 +177,16 @@ def tile_edgeupdaterwrapper_v01_pb_t_kernel(
                     nc.tensor.transpose(
                         p_t[:, c, P * m : P * (m + 1)], p_all[:, 2 * pair + m, P * c : P * (c + 1)], ident_bf16[:]
                     )
-            hid_grouped = work.tile([P, 2, P, PACK], BF16, align_bytes=64, bufs=4)
+            if pair % 2 == 0:
+                hid_grouped = work.tile([P, 2, 2, P, PACK], BF16, align_bytes=64)
+                grouped_of[pair // 2] = hid_grouped
             nc.scalar.copy(
-                out=hid_grouped[:]
+                out=grouped_of[pair // 2][:, pair % 2]
                 .rearrange("p n q t -> p (n q t)")
                 .bitcast(F32)
                 .rearrange("p (n q u) -> p n q u", n=2, u=2),
                 in_=word_t[:].rearrange("p n u q -> p n q u"),
             )
-            grouped_of[pair] = hid_grouped
             for c in range(P_SLABS):
                 nc.scalar.activation(
                     out=operand_of[b][2][:, c, 2 * P * local : 2 * P * (local + 1)],
@@ -191,13 +195,13 @@ def tile_edgeupdaterwrapper_v01_pb_t_kernel(
                     bias=b2_cols[:, 2 * X_SLABS + c : 2 * X_SLABS + c + 1],
                 )
 
-        def quantise_hid_pair(pair):
-            b, local = divmod(pair, PAIRS_PER_BLOCK)
-            cols = slice(2 * P * local, 2 * P * (local + 1))
+        def quantise_hid(half):
+            b, h = divmod(half, HALVES)
+            cols = slice(N_MAX * h, N_MAX * (h + 1))
             nc.vector.quantize_mx(
                 out=operand_of[b][0][:, cols].bitcast(FP8X4),
                 scales=operand_of[b][1][:, cols],
-                in_=grouped_of[pair][:].rearrange("p n q t -> p (n q t)"),
+                in_=grouped_of[half][:].rearrange("p m n q t -> p (m n q t)"),
             )
 
         def first_matmul(b, c):
@@ -216,68 +220,69 @@ def tile_edgeupdaterwrapper_v01_pb_t_kernel(
                 )
                 product_of[(b, c, h)] = product
 
-        def make_s(b, c):
-            b2_plus_p = operand_of[b][2]
-            if c == 0:
+        def make_s(b, c, h):
+            if c == 0 and h == 0:
                 s_planes = blocks.tile([P, PASSES, PACK, BLOCK], BF16, bufs=3)
                 planes_of[b] = s_planes
-            s_slab = work.tile([P, BLOCK], BF16, bufs=4)
-            for h in range(HALVES):
-                cols = slice(N_MAX * h, N_MAX * (h + 1))
-                first_i = (BLOCK * b + N_MAX * h) // NODES
-                if c < X_SLABS:
-                    b2_plus_z = (
-                        b2_plus_xi[:, c, first_i : first_i + I_PER_HALF]
-                        .unsqueeze(2)
-                        .to_broadcast([P, I_PER_HALF, NODES])
-                    )
-                elif c < 2 * X_SLABS:
-                    b2_plus_z = b2_plus_xj[:, c - X_SLABS, :].unsqueeze(1).to_broadcast([P, I_PER_HALF, NODES])
-                else:
-                    b2_plus_z = b2_plus_p[:, c - 2 * X_SLABS, cols].rearrange("f (i j) -> f i j", j=NODES)
-                nc.vector.scalar_tensor_tensor(
-                    out=s_slab[:, cols].rearrange("f (i j) -> f i j", j=NODES),
-                    in0=product_of[(b, c, h)][:].rearrange("f (i j) -> f i j", j=NODES),
-                    scalar=neg_b2_cols[:, c : c + 1],
-                    in1=b2_plus_z,
-                    op0=ALU.max,
-                    op1=ALU.add,
+            if h == 0:
+                s_slab = work.tile([P, BLOCK], BF16, bufs=4)
+                slab_of[(b, c)] = s_slab
+            cols = slice(N_MAX * h, N_MAX * (h + 1))
+            first_i = (BLOCK * b + N_MAX * h) // NODES
+            if c < X_SLABS:
+                b2_plus_z = (
+                    b2_plus_xi[:, c, first_i : first_i + I_PER_HALF].unsqueeze(2).to_broadcast([P, I_PER_HALF, NODES])
                 )
+            elif c < 2 * X_SLABS:
+                b2_plus_z = b2_plus_xj[:, c - X_SLABS, :].unsqueeze(1).to_broadcast([P, I_PER_HALF, NODES])
+            else:
+                b2_plus_z = operand_of[b][2][:, c - 2 * X_SLABS, cols].rearrange("f (i j) -> f i j", j=NODES)
+            nc.vector.scalar_tensor_tensor(
+                out=slab_of[(b, c)][:, cols].rearrange("f (i j) -> f i j", j=NODES),
+                in0=product_of[(b, c, h)][:].rearrange("f (i j) -> f i j", j=NODES),
+                scalar=neg_b2_cols[:, c : c + 1],
+                in1=b2_plus_z,
+                op0=ALU.max,
+                op1=ALU.add,
+            )
+
+        def regroup_partitions(b, c):
             first_p = WORD_ROWS * (c % SLABS_PER_PASS)
             for t in range(PACK):
                 nc.sync.dma_start(
                     out=planes_of[b][first_p : first_p + WORD_ROWS, c // SLABS_PER_PASS, t, :],
-                    in_=s_slab[t:P:PACK, :],
+                    in_=slab_of[(b, c)][t:P:PACK, :],
                 )
 
-        def group_tile(tile, copy):
+        def group_tile(tile):
             b, n = divmod(tile, TILES)
-            s_grouped = work.tile([P, PASSES, P, PACK], BF16, align_bytes=64, bufs=6)
+            if tile % 2 == 0:
+                s_grouped = work.tile([P, 2, PASSES, P, PACK], BF16, align_bytes=64)
+                s_grouped_of[tile // 2] = s_grouped
             for g in range(PASSES):
-                copy(
-                    out=s_grouped[:, g].rearrange("p (c i) t -> p c t i", i=4),
+                nc.scalar.copy(
+                    out=s_grouped_of[tile // 2][:, tile % 2, g].rearrange("p (c i) t -> p c t i", i=4),
                     in_=planes_of[b][:, g, :, P * n : P * (n + 1)].rearrange("p t (c i) -> p c t i", i=4),
                 )
-            s_grouped_of[tile] = s_grouped
 
-        def quantise_s(tile):
-            s_codes = work.tile([P, PASSES, P], U32, align_bytes=64)
-            s_scales = work.tile([P, PASSES, P], U8, align_bytes=64)
+        def quantise_s(pair):
+            s_codes = work.tile([P, 2, PASSES, P], U32, align_bytes=64)
+            s_scales = work.tile([P, 2, PASSES, P], U8, align_bytes=64)
             nc.vector.quantize_mx(
-                out=s_codes[:].rearrange("p g q -> p (g q)").bitcast(FP8X4),
-                scales=s_scales[:].rearrange("p g q -> p (g q)"),
-                in_=s_grouped_of[tile][:].rearrange("p g q t -> p (g q t)"),
+                out=s_codes[:].rearrange("p n g q -> p (n g q)").bitcast(FP8X4),
+                scales=s_scales[:].rearrange("p n g q -> p (n g q)"),
+                in_=s_grouped_of[pair][:].rearrange("p n g q t -> p (n g q t)"),
             )
-            s_codes_of[tile] = (s_codes, s_scales)
+            s_codes_of[pair] = (s_codes, s_scales)
 
         def second_matmul(tile):
-            s_codes, s_scales = s_codes_of[tile]
+            s_codes, s_scales = s_codes_of[tile // 2]
             y = psum.tile([P, ED], F32, tag="y", bufs=2)
             for g in range(PASSES):
                 nc.tensor.matmul_mx(
                     out=y[:],
-                    lhsT=s_codes[:, g, :].bitcast(FP8X4),
-                    lhsT_scale=s_scales[:, g, :],
+                    lhsT=s_codes[:, tile % 2, g, :].bitcast(FP8X4),
+                    lhsT_scale=s_scales[:, tile % 2, g, :],
                     rhs=wo_words[:, g, :].bitcast(FP8X4),
                     rhs_scale=wo_scales[:, g, :],
                     start=(g == 0),
@@ -287,51 +292,52 @@ def tile_edgeupdaterwrapper_v01_pb_t_kernel(
 
         def add_bo(tile):
             z = work.tile([P, ED], F32, bufs=6)
-            z_sum = stats.tile([P, 1], F32)
-            nc.vector.scalar_tensor_tensor(
-                out=z[:], in0=y_of[tile][:], scalar=0.0, in1=bo_rows[:], op0=ALU.add, op1=ALU.add, accum_out=z_sum[:]
-            )
-            z_of[tile] = (z, z_sum)
+            nc.vector.tensor_tensor(out=z[:], in0=y_of[tile][:], in1=bo_rows[:], op=ALU.add)
+            z_of[tile] = z
 
-        def row_statistics(tile):
-            z, z_sum = z_of[tile]
-            neg_mean = stats.tile([P, 1], F32, bufs=8)
-            nc.scalar.mul(out=neg_mean[:], in_=z_sum[:], mul=-1.0 / ED)
-            unused = work.tile([P, ED], F32, bufs=2)
-            sq_sum = stats.tile([P, 1], F32)
-            nc.scalar.activation(
-                out=unused[:], in_=z[:], func=ACT.Square, bias=neg_mean[:], accum_out=sq_sum[:]
-            )
+        def row_sums(tile):
+            sums = stats.tile([P, 6], F32)
+            nc.vector.bn_stats(out=sums[:], in_=z_of[tile][:])
+            sums_of[tile] = sums
+
+        def mean_and_variance(tile):
+            mean_var = stats.tile([P, 2], F32, bufs=8)
+            nc.vector.bn_aggr(out=mean_var[:], in_=sums_of[tile][:])
+            mean_var_of[tile] = mean_var
+
+        def inverse_deviation(tile):
             rstd = stats.tile([P, 1], F32, bufs=8)
             nc.scalar.activation(
-                out=rstd[:], in_=sq_sum[:], func=ACT.Abs_reciprocal_sqrt, scale=1.0 / ED, bias=eps_col[:]
+                out=rstd[:], in_=mean_var_of[tile][:, 1:2], func=ACT.Abs_reciprocal_sqrt, bias=eps_col[:]
             )
-            stats_of[tile] = (neg_mean, rstd)
+            rstd_of[tile] = rstd
 
-        def apply_gain(tile):
-            centred = work.tile([P, ED], F32)
-            nc.vector.scalar_tensor_tensor(
-                out=centred[:],
-                in0=z_of[tile][0][:],
-                scalar=stats_of[tile][0][:],
-                in1=gain_rows[:],
-                op0=ALU.add,
+        def normalise(tile):
+            if tile % 2 == 0:
+                normed = work.tile([P, 2, ED], F32)
+                normed_of[tile // 2] = normed
+            nc.gpsimd.tensor_scalar(
+                out=normed_of[tile // 2][:, tile % 2, :],
+                in0=z_of[tile][:],
+                scalar1=mean_var_of[tile][:, 0:1],
+                scalar2=rstd_of[tile][:],
+                op0=ALU.subtract,
                 op1=ALU.mult,
             )
-            centred_of[tile] = centred
 
-        def add_residual(tile):
-            if tile % 2 == 0:
-                result = work.tile([P, 2, ED], F32, bufs=4)
-                result_of[tile // 2] = result
-            nc.vector.scalar_tensor_tensor(
-                out=result_of[tile // 2][:, tile % 2, :],
-                in0=centred_of[tile][:],
-                scalar=stats_of[tile][1][:],
-                in1=residual_all[:, tile, :],
-                op0=ALU.mult,
-                op1=ALU.add,
+        def finish_pair(pair):
+            scaled = work.tile([P, 2, ED], F32)
+            nc.gpsimd.tensor_tensor(
+                out=scaled[:],
+                in0=normed_of[pair][:],
+                in1=gain_rows[:].unsqueeze(1).to_broadcast([P, 2, ED]),
+                op=ALU.mult,
             )
+            result = work.tile([P, 2, ED], F32)
+            nc.gpsimd.tensor_tensor(
+                out=result[:], in0=scaled[:], in1=residual_all[:, 2 * pair : 2 * pair + 2, :], op=ALU.add
+            )
+            result_of[pair] = result
 
         def store_pair(pair):
             nc.sync.dma_start(
@@ -339,43 +345,42 @@ def tile_edgeupdaterwrapper_v01_pb_t_kernel(
                 in_=result_of[pair][:],
             )
 
-        def grouped_by_scalar(tile):
-            return tile + SLAB_LEAD < ALL_TILES
-
         load_block(0)
         load_block(1)
         with tc.manual_schedule():
             for step in range(-PAIR_LEAD, ALL_TILES + 2 + LAG + 1):
-                done = step - 1 - LAG
                 if (step + LOAD_LEAD) % TILES == 0 and 2 <= (step + LOAD_LEAD) // TILES < BLOCKS:
                     load_block((step + LOAD_LEAD) // TILES)
-                if (step + PAIR_LEAD - LAG) % 2 == 0 and 0 <= (step + PAIR_LEAD - LAG) // 2 < ALL_PAIRS:
-                    quantise_hid_pair((step + PAIR_LEAD - LAG) // 2)
-                if 0 <= step < ALL_TILES and not grouped_by_scalar(step):
-                    group_tile(step, nc.vector.tensor_copy)
-                if 0 <= done < ALL_TILES:
-                    apply_gain(done)
-                if 0 <= step < ALL_TILES:
-                    quantise_s(step)
+                half_step = step + PAIR_LEAD - LAG - 2
+                if half_step % 4 == 0 and 0 <= half_step // 4 < BLOCKS * HALVES:
+                    quantise_hid(half_step // 4)
+                if step % 2 == 0 and 0 <= step < ALL_TILES:
+                    quantise_s(step // 2)
                 if 0 <= step + SLAB_LEAD + 1 < ALL_TILES:
-                    b, k = divmod(step + SLAB_LEAD + 1, TILES)
-                    for c in range(SLABS_PER_STEP * k, SLABS_PER_STEP * (k + 1)):
-                        first_matmul(b, c)
+                    first_matmul((step + SLAB_LEAD + 1) // TILES, (step + SLAB_LEAD + 1) % TILES)
                 if 0 <= step < ALL_TILES:
                     second_matmul(step)
+                slabs_left = 0 <= step + SLAB_LEAD < ALL_TILES
+                b, c = divmod(step + SLAB_LEAD, TILES)
                 if 0 <= step - 1 < ALL_TILES:
                     add_bo(step - 1)
-                if 0 <= step + SLAB_LEAD < ALL_TILES:
-                    b, k = divmod(step + SLAB_LEAD, TILES)
-                    for c in range(SLABS_PER_STEP * k, SLABS_PER_STEP * (k + 1)):
-                        make_s(b, c)
-                if 0 <= done < ALL_TILES:
-                    add_residual(done)
-                    if done % 2 == 1:
-                        store_pair(done // 2)
+                if slabs_left:
+                    make_s(b, c, 0)
                 if 0 <= step - 1 < ALL_TILES:
-                    row_statistics(step - 1)
-                if 0 <= step + LAG < ALL_TILES and grouped_by_scalar(step + LAG):
-                    group_tile(step + LAG, nc.scalar.copy)
+                    row_sums(step - 1)
+                if slabs_left:
+                    make_s(b, c, 1)
+                    regroup_partitions(b, c)
+                if 0 <= step - 1 < ALL_TILES:
+                    mean_and_variance(step - 1)
+                if 0 <= step - 2 < ALL_TILES:
+                    inverse_deviation(step - 2)
+                    normalise(step - 2)
+                    if step % 2 == 1:
+                        finish_pair((step - 2) // 2)
+                if 0 <= step + LAG + 1 < ALL_TILES:
+                    group_tile(step + LAG + 1)
                 if (step + PAIR_LEAD) % 2 == 0 and 0 <= (step + PAIR_LEAD) // 2 < ALL_PAIRS:
                     transpose_pair((step + PAIR_LEAD) // 2)
+                if (step - LAG) % 2 == 1 and 0 <= (step - LAG - 2) // 2 < ALL_PAIRS:
+                    store_pair((step - LAG - 2) // 2)

@@ -54,11 +54,57 @@ def tile_edgeupdaterwrapper_v01_pb_t_kernel(
 
     with tc.tile_pool(name="consts", bufs=1) as consts, tc.tile_pool(name="blocks", bufs=2) as blocks, tc.tile_pool(
         name="work", bufs=3
-    ) as work, tc.tile_pool(name="stats", bufs=4) as stats, tc.psum_pool(name="psum", bufs=2) as psum:
+    ) as work, tc.tile_pool(name="stats", bufs=4) as stats, tc.psum_pool(
+        name="psum", bufs=2
+    ) as psum, tc.manual_schedule():
+
+        hid_of = {}
+        operand_of = {}
+        grouped_of = {}
+        product_of = {}
+        slab_of = {}
+        planes_of = {}
+        s_grouped_of = {}
+        s_codes_of = {}
+        y_of = {}
+        z_of = {}
+        stats_of = {}
+        centred_of = {}
+        result_of = {}
+
+        p_all = consts.tile([P, ALL_TILES, ED], BF16)
+        residual_all = consts.tile([P, ALL_TILES, ED], F32)
+        beta_rows = consts.tile([P, ED], BF16)
+
+        def load_hid(b, pairs):
+            if b not in hid_of:
+                hid_rows = blocks.tile([P, TILES, F], BF16)
+                hid_of[b] = hid_rows
+            for local in pairs:
+                first_row = BLOCK * b + 2 * P * local
+                nc.sync.dma_start(
+                    out=hid_of[b][:, 2 * local : 2 * local + 2, :],
+                    in_=hid_rows_all[first_row : first_row + 2 * P, :].rearrange("(n q) k -> q n k", q=P),
+                )
+
+        def load_p(b):
+            tiles = slice(TILES * b, TILES * (b + 1))
+            nc.sync.dma_start(
+                out=p_all[:, tiles, :],
+                in_=p_rows_all[BLOCK * b : BLOCK * (b + 1), :].rearrange("(n q) d -> q n d", q=P),
+            )
+            nc.gpsimd.tensor_tensor(
+                out=residual_all[:, tiles, :],
+                in0=p_all[:, tiles, :],
+                in1=beta_rows[:].unsqueeze(1).to_broadcast([P, TILES, ED]),
+                op=ALU.add,
+            )
+
         w2_scales = consts.tile([P, MD], U8, align_bytes=64)
         wo_scales = consts.tile([P, PASSES, ED], U8, align_bytes=64)
         nc.vector.memset(w2_scales[:].bitcast(I32), 0)
         nc.vector.memset(wo_scales[:].rearrange("p g n -> p (g n)").bitcast(I32), 0)
+        load_hid(0, range(0, PAIRS_PER_BLOCK // 2))
         for quad in range(4):
             nc.sync.dma_start(
                 out=w2_scales[32 * quad : 32 * quad + 4, :].bitcast(I32),
@@ -68,6 +114,28 @@ def tile_edgeupdaterwrapper_v01_pb_t_kernel(
         nc.sync.dma_start(
             out=w2_words[:].bitcast(I32), in_=W2_words.rearrange("g p n t -> (g p) (n t)").bitcast(I32)
         )
+        load_hid(0, range(PAIRS_PER_BLOCK // 2, PAIRS_PER_BLOCK))
+
+        b2_stage = consts.tile([P, P], BF16)
+        nc.vector.memset(b2_stage[:], 0.0)
+        nc.scalar.dma_start(out=b2_stage[0:SLABS, :], in_=b2.rearrange("(c f) -> c f", f=P))
+        x_stage = consts.tile([P, HD], BF16)
+        nc.vector.memset(x_stage[NODES:P, :], 0.0)
+        nc.scalar.dma_start(out=x_stage[0:NODES, :], in_=x_down.rearrange("b n d -> (b n) d"))
+        nc.scalar.dma_start(out=beta_rows[:], in_=ln_out_b.partition_broadcast(P))
+        bo_rows = consts.tile([P, ED], BF16)
+        nc.scalar.dma_start(out=bo_rows[:], in_=bo.partition_broadcast(P))
+        gain_rows = consts.tile([P, ED], BF16)
+        nc.scalar.dma_start(out=gain_rows[:], in_=ln_out_g.partition_broadcast(P))
+        eps_col = consts.tile([P, 1], F32)
+        nc.vector.memset(eps_col[:], EPS)
+
+        ident_f32 = consts.tile([P, P], F32)
+        make_identity(nc, ident_f32[:])
+        ident_bf16 = consts.tile([P, P], BF16)
+        make_identity(nc, ident_bf16[:])
+
+        load_p(0)
         for quad in range(4):
             nc.sync.dma_start(
                 out=wo_scales[32 * quad : 32 * quad + 4, :, :].bitcast(I32),
@@ -77,24 +145,9 @@ def tile_edgeupdaterwrapper_v01_pb_t_kernel(
         nc.sync.dma_start(
             out=wo_words[:].bitcast(I32), in_=Wo_words.rearrange("g p n t -> p g (n t)").bitcast(I32)
         )
+        load_hid(1, range(PAIRS_PER_BLOCK))
+        load_p(1)
 
-        ident_f32 = consts.tile([P, P], F32)
-        make_identity(nc, ident_f32[:])
-        ident_bf16 = consts.tile([P, P], BF16)
-        make_identity(nc, ident_bf16[:])
-        eps_col = consts.tile([P, 1], F32)
-        nc.vector.memset(eps_col[:], EPS)
-
-        bo_rows = consts.tile([P, ED], BF16)
-        nc.scalar.dma_start(out=bo_rows[:], in_=bo.partition_broadcast(P))
-        gain_rows = consts.tile([P, ED], BF16)
-        nc.scalar.dma_start(out=gain_rows[:], in_=ln_out_g.partition_broadcast(P))
-        beta_rows = consts.tile([P, ED], BF16)
-        nc.scalar.dma_start(out=beta_rows[:], in_=ln_out_b.partition_broadcast(P))
-
-        b2_stage = consts.tile([P, P], BF16)
-        nc.vector.memset(b2_stage[:], 0.0)
-        nc.scalar.dma_start(out=b2_stage[0:SLABS, :], in_=b2.rearrange("(c f) -> c f", f=P))
         b2_t = psum.tile([P, P], BF16, tag="from_rows", bufs=1)
         nc.tensor.transpose(b2_t[:], b2_stage[:], ident_bf16[:])
         b2_cols = consts.tile([P, SLABS], F32)
@@ -104,9 +157,6 @@ def tile_edgeupdaterwrapper_v01_pb_t_kernel(
             out=neg_b2_cols[:], in0=b2_t[:, 0:SLABS], scalar1=-1.0, scalar2=None, op0=ALU.mult
         )
 
-        x_stage = consts.tile([P, HD], BF16)
-        nc.vector.memset(x_stage[NODES:P, :], 0.0)
-        nc.scalar.dma_start(out=x_stage[0:NODES, :], in_=x_down.rearrange("b n d -> (b n) d"))
         x_t = psum.tile([P, X_SLABS, P], BF16, tag="from_rows", bufs=1)
         for c in range(X_SLABS):
             nc.tensor.transpose(x_t[:, c, :], x_stage[:, P * c : P * (c + 1)], ident_bf16[:])
@@ -121,42 +171,6 @@ def tile_edgeupdaterwrapper_v01_pb_t_kernel(
                 in_=x_t[:, c, 0:NODES],
                 func=ACT.Identity,
                 bias=b2_cols[:, X_SLABS + c : X_SLABS + c + 1],
-            )
-
-
-        p_all = consts.tile([P, ALL_TILES, ED], BF16)
-        residual_all = consts.tile([P, ALL_TILES, ED], F32)
-
-        hid_of = {}
-        operand_of = {}
-        grouped_of = {}
-        product_of = {}
-        planes_of = {}
-        y_of = {}
-        s_grouped_of = {}
-        s_codes_of = {}
-        z_of = {}
-        slab_of = {}
-        sums_of = {}
-        mean_var_of = {}
-        rstd_of = {}
-        normed_of = {}
-        result_of = {}
-
-        def load_block(b):
-            rows = slice(BLOCK * b, BLOCK * (b + 1))
-            hid_rows = blocks.tile([P, TILES, F], BF16)
-            nc.sync.dma_start(out=hid_rows[:], in_=hid_rows_all[rows, :].rearrange("(n q) k -> q n k", q=P))
-            nc.sync.dma_start(
-                out=p_all[:, TILES * b : TILES * (b + 1), :],
-                in_=p_rows_all[rows, :].rearrange("(n q) d -> q n d", q=P),
-            )
-            hid_of[b] = hid_rows
-            nc.gpsimd.tensor_tensor(
-                out=residual_all[:, TILES * b : TILES * (b + 1), :],
-                in0=p_all[:, TILES * b : TILES * (b + 1), :],
-                in1=beta_rows[:].unsqueeze(1).to_broadcast([P, TILES, ED]),
-                op=ALU.add,
             )
 
         def transpose_pair(pair):
@@ -225,7 +239,7 @@ def tile_edgeupdaterwrapper_v01_pb_t_kernel(
                 s_planes = blocks.tile([P, PASSES, PACK, BLOCK], BF16, bufs=3)
                 planes_of[b] = s_planes
             if h == 0:
-                s_slab = work.tile([P, BLOCK], BF16, bufs=4)
+                s_slab = work.tile([P, BLOCK], BF16, bufs=6)
                 slab_of[(b, c)] = s_slab
             cols = slice(N_MAX * h, N_MAX * (h + 1))
             first_i = (BLOCK * b + N_MAX * h) // NODES
@@ -254,13 +268,13 @@ def tile_edgeupdaterwrapper_v01_pb_t_kernel(
                     in_=slab_of[(b, c)][t:P:PACK, :],
                 )
 
-        def group_tile(tile):
+        def group_tile(tile, copy):
             b, n = divmod(tile, TILES)
-            if tile % 2 == 0:
-                s_grouped = work.tile([P, 2, PASSES, P, PACK], BF16, align_bytes=64)
+            if tile // 2 not in s_grouped_of:
+                s_grouped = work.tile([P, 2, PASSES, P, PACK], BF16, align_bytes=64, bufs=4)
                 s_grouped_of[tile // 2] = s_grouped
             for g in range(PASSES):
-                nc.scalar.copy(
+                copy(
                     out=s_grouped_of[tile // 2][:, tile % 2, g].rearrange("p (c i) t -> p c t i", i=4),
                     in_=planes_of[b][:, g, :, P * n : P * (n + 1)].rearrange("p t (c i) -> p c t i", i=4),
                 )
@@ -292,52 +306,51 @@ def tile_edgeupdaterwrapper_v01_pb_t_kernel(
 
         def add_bo(tile):
             z = work.tile([P, ED], F32, bufs=6)
-            nc.vector.tensor_tensor(out=z[:], in0=y_of[tile][:], in1=bo_rows[:], op=ALU.add)
-            z_of[tile] = z
+            z_sum = stats.tile([P, 1], F32)
+            nc.vector.scalar_tensor_tensor(
+                out=z[:], in0=y_of[tile][:], scalar=0.0, in1=bo_rows[:], op0=ALU.add, op1=ALU.add, accum_out=z_sum[:]
+            )
+            z_of[tile] = (z, z_sum)
 
-        def row_sums(tile):
-            sums = stats.tile([P, 6], F32)
-            nc.vector.bn_stats(out=sums[:], in_=z_of[tile][:])
-            sums_of[tile] = sums
-
-        def mean_and_variance(tile):
-            mean_var = stats.tile([P, 2], F32, bufs=8)
-            nc.vector.bn_aggr(out=mean_var[:], in_=sums_of[tile][:])
-            mean_var_of[tile] = mean_var
-
-        def inverse_deviation(tile):
+        def row_statistics(tile):
+            z, z_sum = z_of[tile]
+            neg_mean = stats.tile([P, 1], F32, bufs=8)
+            nc.scalar.mul(out=neg_mean[:], in_=z_sum[:], mul=-1.0 / ED)
+            unused = work.tile([P, ED], F32, bufs=2)
+            sq_sum = stats.tile([P, 1], F32)
+            nc.scalar.activation(
+                out=unused[:], in_=z[:], func=ACT.Square, bias=neg_mean[:], accum_out=sq_sum[:]
+            )
             rstd = stats.tile([P, 1], F32, bufs=8)
             nc.scalar.activation(
-                out=rstd[:], in_=mean_var_of[tile][:, 1:2], func=ACT.Abs_reciprocal_sqrt, bias=eps_col[:]
+                out=rstd[:], in_=sq_sum[:], func=ACT.Abs_reciprocal_sqrt, scale=1.0 / ED, bias=eps_col[:]
             )
-            rstd_of[tile] = rstd
+            stats_of[tile] = (neg_mean, rstd)
 
-        def normalise(tile):
-            if tile % 2 == 0:
-                normed = work.tile([P, 2, ED], F32)
-                normed_of[tile // 2] = normed
-            nc.gpsimd.tensor_scalar(
-                out=normed_of[tile // 2][:, tile % 2, :],
-                in0=z_of[tile][:],
-                scalar1=mean_var_of[tile][:, 0:1],
-                scalar2=rstd_of[tile][:],
-                op0=ALU.subtract,
+        def apply_gain(tile):
+            centred = work.tile([P, ED], F32)
+            nc.vector.scalar_tensor_tensor(
+                out=centred[:],
+                in0=z_of[tile][0][:],
+                scalar=stats_of[tile][0][:],
+                in1=gain_rows[:],
+                op0=ALU.add,
                 op1=ALU.mult,
             )
+            centred_of[tile] = centred
 
-        def finish_pair(pair):
-            scaled = work.tile([P, 2, ED], F32)
-            nc.gpsimd.tensor_tensor(
-                out=scaled[:],
-                in0=normed_of[pair][:],
-                in1=gain_rows[:].unsqueeze(1).to_broadcast([P, 2, ED]),
-                op=ALU.mult,
+        def add_residual(tile):
+            if tile % 2 == 0:
+                result = work.tile([P, 2, ED], F32, bufs=4)
+                result_of[tile // 2] = result
+            nc.vector.scalar_tensor_tensor(
+                out=result_of[tile // 2][:, tile % 2, :],
+                in0=centred_of[tile][:],
+                scalar=stats_of[tile][1][:],
+                in1=residual_all[:, tile, :],
+                op0=ALU.mult,
+                op1=ALU.add,
             )
-            result = work.tile([P, 2, ED], F32)
-            nc.gpsimd.tensor_tensor(
-                out=result[:], in0=scaled[:], in1=residual_all[:, 2 * pair : 2 * pair + 2, :], op=ALU.add
-            )
-            result_of[pair] = result
 
         def store_pair(pair):
             nc.sync.dma_start(
@@ -345,42 +358,41 @@ def tile_edgeupdaterwrapper_v01_pb_t_kernel(
                 in_=result_of[pair][:],
             )
 
-        load_block(0)
-        load_block(1)
-        with tc.manual_schedule():
-            for step in range(-PAIR_LEAD, ALL_TILES + 2 + LAG + 1):
-                if (step + LOAD_LEAD) % TILES == 0 and 2 <= (step + LOAD_LEAD) // TILES < BLOCKS:
-                    load_block((step + LOAD_LEAD) // TILES)
-                half_step = step + PAIR_LEAD - LAG - 2
-                if half_step % 4 == 0 and 0 <= half_step // 4 < BLOCKS * HALVES:
-                    quantise_hid(half_step // 4)
-                if step % 2 == 0 and 0 <= step < ALL_TILES:
-                    quantise_s(step // 2)
-                if 0 <= step + SLAB_LEAD + 1 < ALL_TILES:
-                    first_matmul((step + SLAB_LEAD + 1) // TILES, (step + SLAB_LEAD + 1) % TILES)
-                if 0 <= step < ALL_TILES:
-                    second_matmul(step)
-                slabs_left = 0 <= step + SLAB_LEAD < ALL_TILES
+        def grouped_by_scalar(tile):
+            return tile + SLAB_LEAD < ALL_TILES or tile % 2 == 1
+
+        for step in range(-PAIR_LEAD, ALL_TILES + 2 + LAG + 1):
+            done = step - 1 - LAG
+            if (step + LOAD_LEAD) % TILES == 0 and 2 <= (step + LOAD_LEAD) // TILES < BLOCKS:
+                load_hid((step + LOAD_LEAD) // TILES, range(PAIRS_PER_BLOCK))
+                load_p((step + LOAD_LEAD) // TILES)
+            half_step = step + PAIR_LEAD - LAG - 2
+            if half_step % 4 == 0 and 0 <= half_step // 4 < BLOCKS * HALVES:
+                quantise_hid(half_step // 4)
+            if 0 <= step < ALL_TILES and not grouped_by_scalar(step):
+                group_tile(step, nc.vector.tensor_copy)
+            if 0 <= done < ALL_TILES:
+                apply_gain(done)
+            if step % 2 == 0 and 0 <= step < ALL_TILES:
+                quantise_s(step // 2)
+            if 0 <= step + SLAB_LEAD + 1 < ALL_TILES:
+                first_matmul((step + SLAB_LEAD + 1) // TILES, (step + SLAB_LEAD + 1) % TILES)
+            if 0 <= step < ALL_TILES:
+                second_matmul(step)
+            if 0 <= step - 1 < ALL_TILES:
+                add_bo(step - 1)
+            if 0 <= step + SLAB_LEAD < ALL_TILES:
                 b, c = divmod(step + SLAB_LEAD, TILES)
-                if 0 <= step - 1 < ALL_TILES:
-                    add_bo(step - 1)
-                if slabs_left:
-                    make_s(b, c, 0)
-                if 0 <= step - 1 < ALL_TILES:
-                    row_sums(step - 1)
-                if slabs_left:
-                    make_s(b, c, 1)
-                    regroup_partitions(b, c)
-                if 0 <= step - 1 < ALL_TILES:
-                    mean_and_variance(step - 1)
-                if 0 <= step - 2 < ALL_TILES:
-                    inverse_deviation(step - 2)
-                    normalise(step - 2)
-                    if step % 2 == 1:
-                        finish_pair((step - 2) // 2)
-                if 0 <= step + LAG + 1 < ALL_TILES:
-                    group_tile(step + LAG + 1)
-                if (step + PAIR_LEAD) % 2 == 0 and 0 <= (step + PAIR_LEAD) // 2 < ALL_PAIRS:
-                    transpose_pair((step + PAIR_LEAD) // 2)
-                if (step - LAG) % 2 == 1 and 0 <= (step - LAG - 2) // 2 < ALL_PAIRS:
-                    store_pair((step - LAG - 2) // 2)
+                for h in range(HALVES):
+                    make_s(b, c, h)
+                regroup_partitions(b, c)
+            if 0 <= done < ALL_TILES:
+                add_residual(done)
+                if done % 2 == 1:
+                    store_pair(done // 2)
+            if 0 <= step - 1 < ALL_TILES:
+                row_statistics(step - 1)
+            if 0 <= step + LAG + 1 < ALL_TILES and grouped_by_scalar(step + LAG + 1):
+                group_tile(step + LAG + 1, nc.scalar.copy)
+            if (step + PAIR_LEAD) % 2 == 0 and 0 <= (step + PAIR_LEAD) // 2 < ALL_PAIRS:
+                transpose_pair((step + PAIR_LEAD) // 2)

@@ -12,33 +12,28 @@ ACT = mybir.ActivationFunctionType
 
 P = 128
 PACK = 4
-K_PASS = P * PACK
-N_MAX = 512
 NODES = 64
 HD = 384
 ED = 256
 F = 512
 MD = HD + HD + ED
+K_PASS = P * PACK
 PASSES = MD // K_PASS
-SLABS = MD // P
-SLABS_PER_PASS = SLABS // PASSES
-X_SLABS = HD // P
-P_SLABS = ED // P
-WORD_ROWS = P // PACK
+SLABS = PASSES * PACK
 ROWS = NODES * NODES
-BLOCK = 1024
-BLOCKS = ROWS // BLOCK
-HALVES = BLOCK // N_MAX
-TILES = BLOCK // P
-ALL_TILES = ROWS // P
-PAIRS_PER_BLOCK = TILES // 2
-ALL_PAIRS = ALL_TILES // 2
-assert SLABS == TILES
-LAG = 3
-SLAB_LEAD = TILES + LAG + 2
-PAIR_LEAD = SLAB_LEAD + TILES + LAG
-LOAD_LEAD = PAIR_LEAD + TILES
-I_PER_HALF = N_MAX // NODES
+GROUP = 512
+GROUPS = ROWS // GROUP
+HALF = GROUP // 2
+TILES = ROWS // P
+PAIRS = TILES // 2
+TILES_PER_GROUP = GROUP // P
+UNITS = GROUPS * PASSES
+XI_PARTS = HD // PACK
+XJ_HEAD = K_PASS - HD
+XJ_TAIL = HD - XJ_HEAD
+I_PER_GROUP = GROUP // NODES
+I_PER_HALF = HALF // NODES
+LOAD_TILES = 8
 EPS = 1e-5
 
 FLOPS = 2 * ROWS * F * MD + 2 * ROWS * MD * ED
@@ -52,18 +47,15 @@ def tile_edgeupdaterwrapper_v01_pb_t_kernel(
     p_rows_all = p_ln.rearrange("b i j d -> (b i j) d")
     out_rows_all = out.rearrange("b i j d -> (b i j) d")
 
-    with tc.tile_pool(name="consts", bufs=1) as consts, tc.tile_pool(name="blocks", bufs=2) as blocks, tc.tile_pool(
-        name="work", bufs=3
-    ) as work, tc.tile_pool(name="stats", bufs=4) as stats, tc.psum_pool(
-        name="psum", bufs=2
-    ) as psum, tc.manual_schedule():
-
-        hid_of = {}
-        operand_of = {}
-        grouped_of = {}
+    with tc.tile_pool(name="consts", bufs=1) as consts, tc.tile_pool(name="work", bufs=3) as work, tc.tile_pool(
+        name="stats", bufs=4
+    ) as stats, tc.psum_pool(name="psum", bufs=2) as psum, tc.manual_schedule():
+        hid_grouped_of = {}
+        hid_codes_of = {}
+        word_t_of = {}
         product_of = {}
-        slab_of = {}
-        planes_of = {}
+        m_of = {}
+        zt_of = {}
         s_grouped_of = {}
         s_codes_of = {}
         y_of = {}
@@ -72,56 +64,59 @@ def tile_edgeupdaterwrapper_v01_pb_t_kernel(
         centred_of = {}
         result_of = {}
 
-        p_all = consts.tile([P, ALL_TILES, ED], BF16)
-        residual_all = consts.tile([P, ALL_TILES, ED], F32)
+        hid_all = consts.tile([P, TILES, F], BF16)
+        tail_rows = consts.tile([P, TILES, K_PASS], BF16)
+        residual_all = consts.tile([P, TILES, ED], F32)
         beta_rows = consts.tile([P, ED], BF16)
 
-        def load_hid(b, pairs):
-            if b not in hid_of:
-                hid_rows = blocks.tile([P, TILES, F], BF16)
-                hid_of[b] = hid_rows
-            for local in pairs:
-                first_row = BLOCK * b + 2 * P * local
-                nc.sync.dma_start(
-                    out=hid_of[b][:, 2 * local : 2 * local + 2, :],
-                    in_=hid_rows_all[first_row : first_row + 2 * P, :].rearrange("(n q) k -> q n k", q=P),
-                )
-
-        def load_p(b):
-            tiles = slice(TILES * b, TILES * (b + 1))
+        def load_hid(first_tile, count):
             nc.sync.dma_start(
-                out=p_all[:, tiles, :],
-                in_=p_rows_all[BLOCK * b : BLOCK * (b + 1), :].rearrange("(n q) d -> q n d", q=P),
+                out=hid_all[:, first_tile : first_tile + count, :],
+                in_=hid_rows_all[P * first_tile : P * (first_tile + count), :].rearrange("(n q) k -> q n k", q=P),
             )
+
+        def load_tail_rows(first_tile, count):
+            tiles = slice(first_tile, first_tile + count)
+            nc.sync.dma_start(
+                out=tail_rows[:, tiles, XJ_TAIL:K_PASS],
+                in_=p_rows_all[P * first_tile : P * (first_tile + count), :].rearrange("(n q) d -> q n d", q=P),
+            )
+            for half in range(P // NODES):
+                nc.sync.dma_start(
+                    out=tail_rows[NODES * half : NODES * (half + 1), tiles, 0:XJ_TAIL],
+                    in_=x_down[0, :, XJ_HEAD:HD].unsqueeze(1).to_broadcast([NODES, count, XJ_TAIL]),
+                )
             nc.gpsimd.tensor_tensor(
                 out=residual_all[:, tiles, :],
-                in0=p_all[:, tiles, :],
-                in1=beta_rows[:].unsqueeze(1).to_broadcast([P, TILES, ED]),
+                in0=tail_rows[:, tiles, XJ_TAIL:K_PASS],
+                in1=beta_rows[:].unsqueeze(1).to_broadcast([P, count, ED]),
                 op=ALU.add,
             )
 
-        w2_scales = consts.tile([P, MD], U8, align_bytes=64)
+        w2_scales_raw = consts.tile([P, MD], U8, align_bytes=64)
         wo_scales = consts.tile([P, PASSES, ED], U8, align_bytes=64)
-        nc.vector.memset(w2_scales[:].bitcast(I32), 0)
+        head_rows = consts.tile([P, K_PASS], BF16)
+        nc.vector.memset(w2_scales_raw[:].bitcast(I32), 0)
+        nc.vector.memset(head_rows[:], 0.0)
         nc.vector.memset(wo_scales[:].rearrange("p g n -> p (g n)").bitcast(I32), 0)
-        load_hid(0, range(0, PAIRS_PER_BLOCK // 2))
+        load_hid(0, 2)
+        load_hid(2, 2)
         for quad in range(4):
             nc.sync.dma_start(
-                out=w2_scales[32 * quad : 32 * quad + 4, :].bitcast(I32),
+                out=w2_scales_raw[32 * quad : 32 * quad + 4, :].bitcast(I32),
                 in_=W2_scales[0, 4 * quad : 4 * quad + 4, :].bitcast(I32),
             )
-        w2_words = consts.tile([P, MD], U32, align_bytes=64)
+        w2_words_raw = consts.tile([P, MD], U32, align_bytes=64)
         nc.sync.dma_start(
-            out=w2_words[:].bitcast(I32), in_=W2_words.rearrange("g p n t -> (g p) (n t)").bitcast(I32)
+            out=w2_words_raw[:].bitcast(I32), in_=W2_words.rearrange("g p n t -> (g p) (n t)").bitcast(I32)
         )
-        load_hid(0, range(PAIRS_PER_BLOCK // 2, PAIRS_PER_BLOCK))
 
-        b2_stage = consts.tile([P, P], BF16)
-        nc.vector.memset(b2_stage[:], 0.0)
-        nc.scalar.dma_start(out=b2_stage[0:SLABS, :], in_=b2.rearrange("(c f) -> c f", f=P))
-        x_stage = consts.tile([P, HD], BF16)
-        nc.vector.memset(x_stage[NODES:P, :], 0.0)
-        nc.scalar.dma_start(out=x_stage[0:NODES, :], in_=x_down.rearrange("b n d -> (b n) d"))
+        b2_bf16 = consts.tile([P, SLABS], BF16)
+        nc.scalar.dma_start(
+            out=b2_bf16[:].rearrange("p (g t) -> p g t", t=PACK), in_=b2.rearrange("(g p t) -> p g t", g=PASSES, t=PACK)
+        )
+        nc.scalar.dma_start(out=head_rows[0:NODES, 0:HD], in_=x_down[0, :, :])
+        nc.scalar.dma_start(out=head_rows[NODES:P, HD:K_PASS], in_=x_down[0, :, 0:XJ_HEAD])
         nc.scalar.dma_start(out=beta_rows[:], in_=ln_out_b.partition_broadcast(P))
         bo_rows = consts.tile([P, ED], BF16)
         nc.scalar.dma_start(out=bo_rows[:], in_=bo.partition_broadcast(P))
@@ -135,7 +130,31 @@ def tile_edgeupdaterwrapper_v01_pb_t_kernel(
         ident_bf16 = consts.tile([P, P], BF16)
         make_identity(nc, ident_bf16[:])
 
-        load_p(0)
+        selector = consts.tile([P, NODES, NODES], BF16)
+
+        def build_selector(group):
+            nodes = slice(I_PER_GROUP * group, I_PER_GROUP * (group + 1))
+            nc.gpsimd.tensor_scalar(
+                out=selector[0:NODES, nodes, :],
+                in0=ident_bf16[0:NODES, nodes].unsqueeze(2).to_broadcast([NODES, I_PER_GROUP, NODES]),
+                scalar1=1.0,
+                scalar2=0.0,
+                op0=ALU.mult,
+                op1=ALU.add,
+            )
+            nc.gpsimd.tensor_scalar(
+                out=selector[NODES:P, nodes, :],
+                in0=ident_bf16[NODES:P, NODES:P].unsqueeze(1).to_broadcast([NODES, I_PER_GROUP, NODES]),
+                scalar1=1.0,
+                scalar2=0.0,
+                op0=ALU.mult,
+                op1=ALU.add,
+            )
+
+        build_selector(0)
+        build_selector(1)
+        load_tail_rows(0, LOAD_TILES)
+        load_hid(4, 4)
         for quad in range(4):
             nc.sync.dma_start(
                 out=wo_scales[32 * quad : 32 * quad + 4, :, :].bitcast(I32),
@@ -145,170 +164,157 @@ def tile_edgeupdaterwrapper_v01_pb_t_kernel(
         nc.sync.dma_start(
             out=wo_words[:].bitcast(I32), in_=Wo_words.rearrange("g p n t -> p g (n t)").bitcast(I32)
         )
-        load_hid(1, range(PAIRS_PER_BLOCK))
-        load_p(1)
+        for block in range(1, TILES // LOAD_TILES):
+            load_hid(LOAD_TILES * block, 4)
+            build_selector(2 * block)
+            build_selector(2 * block + 1)
+            load_tail_rows(LOAD_TILES * block, LOAD_TILES)
+            load_hid(LOAD_TILES * block + 4, 4)
 
-        b2_t = psum.tile([P, P], BF16, tag="from_rows", bufs=1)
-        nc.tensor.transpose(b2_t[:], b2_stage[:], ident_bf16[:])
         b2_cols = consts.tile([P, SLABS], F32)
-        nc.vector.tensor_copy(out=b2_cols[:], in_=b2_t[:, 0:SLABS])
-        neg_b2_cols = consts.tile([P, SLABS], F32)
-        nc.vector.tensor_scalar(
-            out=neg_b2_cols[:], in0=b2_t[:, 0:SLABS], scalar1=-1.0, scalar2=None, op0=ALU.mult
+        nc.vector.tensor_copy(out=b2_cols[:], in_=b2_bf16[:])
+        head_slabs = consts.tile([P, PACK, P], BF16)
+        nc.vector.tensor_copy(out=head_slabs[:], in_=head_rows[:].rearrange("k (m t) -> k t m", t=PACK))
+        w2_scales = consts.tile([P, MD], U8, align_bytes=64)
+        nc.vector.tensor_copy(
+            out=w2_scales[:].rearrange("p (g t m) -> p g m t", g=PASSES, t=PACK),
+            in_=w2_scales_raw[:].rearrange("p (g m t) -> p g m t", g=PASSES, t=PACK),
+        )
+        w2_words = consts.tile([P, MD], U32, align_bytes=64)
+        nc.vector.tensor_copy(
+            out=w2_words[:].bitcast(I32).rearrange("p (g t m) -> p g t m", g=PASSES, t=PACK),
+            in_=w2_words_raw[:].bitcast(I32).rearrange("p (g m t) -> p g t m", g=PASSES, t=PACK),
         )
 
-        x_t = psum.tile([P, X_SLABS, P], BF16, tag="from_rows", bufs=1)
-        for c in range(X_SLABS):
-            nc.tensor.transpose(x_t[:, c, :], x_stage[:, P * c : P * (c + 1)], ident_bf16[:])
-        b2_plus_xi = consts.tile([P, X_SLABS, NODES], F32)
-        b2_plus_xj = consts.tile([P, X_SLABS, NODES], F32)
-        for c in range(X_SLABS):
-            nc.scalar.activation(
-                out=b2_plus_xi[:, c, :], in_=x_t[:, c, 0:NODES], func=ACT.Identity, bias=b2_cols[:, c : c + 1]
-            )
-            nc.scalar.activation(
-                out=b2_plus_xj[:, c, :],
-                in_=x_t[:, c, 0:NODES],
-                func=ACT.Identity,
-                bias=b2_cols[:, X_SLABS + c : X_SLABS + c + 1],
-            )
-
-        def transpose_pair(pair):
-            b, local = divmod(pair, PAIRS_PER_BLOCK)
-            if local == 0:
-                hid_codes = blocks.tile([P, BLOCK], U32, align_bytes=64, bufs=3)
-                hid_scales = blocks.tile([P, BLOCK], U8, align_bytes=64, bufs=3)
-                b2_plus_p = blocks.tile([P, P_SLABS, BLOCK], F32, bufs=3)
-                operand_of[b] = (hid_codes, hid_scales, b2_plus_p)
+        def transpose_hid(pair):
             word_t = psum.tile([P, 2, 2, P], F32, tag="word_t", bufs=1)
-            for m in range(2):
-                words = hid_of[b][:, 2 * local + m, :].bitcast(F32)
+            for n in range(2):
+                words = hid_all[:, 2 * pair + n, :].bitcast(F32)
                 for u in range(2):
-                    nc.tensor.transpose(word_t[:, m, u, :], words[:, u : F // 2 : 2], ident_f32[:])
-            p_t = psum.tile([P, P_SLABS, 2 * P], BF16, tag="from_rows", bufs=1)
-            for m in range(2):
-                for c in range(P_SLABS):
-                    nc.tensor.transpose(
-                        p_t[:, c, P * m : P * (m + 1)], p_all[:, 2 * pair + m, P * c : P * (c + 1)], ident_bf16[:]
-                    )
+                    nc.tensor.transpose(word_t[:, n, u, :], words[:, u : F // 2 : 2], ident_f32[:])
+            word_t_of[pair] = word_t
+
+        def group_hid(pair):
             if pair % 2 == 0:
-                hid_grouped = work.tile([P, 2, 2, P, PACK], BF16, align_bytes=64)
-                grouped_of[pair // 2] = hid_grouped
+                hid_grouped = work.tile([P, 2, 2, P, PACK], BF16, align_bytes=64, bufs=2)
+                hid_grouped_of[pair // 2] = hid_grouped
             nc.scalar.copy(
-                out=grouped_of[pair // 2][:, pair % 2]
+                out=hid_grouped_of[pair // 2][:, pair % 2]
                 .rearrange("p n q t -> p (n q t)")
                 .bitcast(F32)
                 .rearrange("p (n q u) -> p n q u", n=2, u=2),
-                in_=word_t[:].rearrange("p n u q -> p n q u"),
+                in_=word_t_of[pair][:].rearrange("p n u q -> p n q u"),
             )
-            for c in range(P_SLABS):
-                nc.scalar.activation(
-                    out=operand_of[b][2][:, c, 2 * P * local : 2 * P * (local + 1)],
-                    in_=p_t[:, c, :],
-                    func=ACT.Identity,
-                    bias=b2_cols[:, 2 * X_SLABS + c : 2 * X_SLABS + c + 1],
-                )
 
-        def quantise_hid(half):
-            b, h = divmod(half, HALVES)
-            cols = slice(N_MAX * h, N_MAX * (h + 1))
+        def quantise_hid(group):
+            hid_codes = work.tile([P, GROUP], U32, align_bytes=64)
+            hid_scales = work.tile([P, GROUP], U8, align_bytes=64)
             nc.vector.quantize_mx(
-                out=operand_of[b][0][:, cols].bitcast(FP8X4),
-                scales=operand_of[b][1][:, cols],
-                in_=grouped_of[half][:].rearrange("p m n q t -> p (m n q t)"),
+                out=hid_codes[:].bitcast(FP8X4),
+                scales=hid_scales[:],
+                in_=hid_grouped_of[group][:].rearrange("p m n q t -> p (m n q t)"),
             )
+            hid_codes_of[group] = (hid_codes, hid_scales)
 
-        def first_matmul(b, c):
-            hid_codes, hid_scales = operand_of[b][0:2]
-            for h in range(HALVES):
-                cols = slice(N_MAX * h, N_MAX * (h + 1))
-                product = psum.tile([P, N_MAX], F32, tag="product", bufs=4)
+        def first_matmul(unit):
+            group, g = divmod(unit, PASSES)
+            hid_codes, hid_scales = hid_codes_of[group]
+            for t in range(PACK):
+                cols = slice(P * (PACK * g + t), P * (PACK * g + t + 1))
+                product = psum.tile([P, GROUP], F32, tag="product", bufs=4)
                 nc.tensor.matmul_mx(
                     out=product[:],
-                    lhsT=w2_words[:, P * c : P * (c + 1)].bitcast(FP8X4),
-                    lhsT_scale=w2_scales[:, P * c : P * (c + 1)],
-                    rhs=hid_codes[:, cols].bitcast(FP8X4),
-                    rhs_scale=hid_scales[:, cols],
+                    lhsT=w2_words[:, cols].bitcast(FP8X4),
+                    lhsT_scale=w2_scales[:, cols],
+                    rhs=hid_codes[:].bitcast(FP8X4),
+                    rhs_scale=hid_scales[:],
                     start=True,
                     stop=True,
                 )
-                product_of[(b, c, h)] = product
+                product_of[(unit, t)] = product
 
-        def make_s(b, c, h):
-            if c == 0 and h == 0:
-                s_planes = blocks.tile([P, PASSES, PACK, BLOCK], BF16, bufs=3)
-                planes_of[b] = s_planes
-            if h == 0:
-                s_slab = work.tile([P, BLOCK], BF16, bufs=6)
-                slab_of[(b, c)] = s_slab
-            cols = slice(N_MAX * h, N_MAX * (h + 1))
-            first_i = (BLOCK * b + N_MAX * h) // NODES
-            if c < X_SLABS:
-                b2_plus_z = (
-                    b2_plus_xi[:, c, first_i : first_i + I_PER_HALF].unsqueeze(2).to_broadcast([P, I_PER_HALF, NODES])
-                )
-            elif c < 2 * X_SLABS:
-                b2_plus_z = b2_plus_xj[:, c - X_SLABS, :].unsqueeze(1).to_broadcast([P, I_PER_HALF, NODES])
+        def relu_out_of_psum(unit, t):
+            if t == 0:
+                m = work.tile([P, PACK, GROUP], F32)
+                m_of[unit] = m
+            slab = PACK * (unit % PASSES) + t
+            nc.scalar.activation(
+                out=m_of[unit][:, t, :], in_=product_of[(unit, t)][:], func=ACT.Relu, bias=b2_cols[:, slab : slab + 1]
+            )
+
+        def transpose_z_in(unit, h):
+            group, g = divmod(unit, PASSES)
+            zt = psum.tile([P, PACK, HALF], BF16, tag="zt", bufs=2)
+            if g == 0:
+                first_i = I_PER_GROUP * group + I_PER_HALF * h
+                for t in range(PACK):
+                    nc.tensor.matmul(
+                        out=zt[:, t, :],
+                        lhsT=head_slabs[:, t, :],
+                        rhs=selector[:, first_i : first_i + I_PER_HALF, :].rearrange("k i j -> k (i j)"),
+                        start=True,
+                        stop=True,
+                    )
             else:
-                b2_plus_z = operand_of[b][2][:, c - 2 * X_SLABS, cols].rearrange("f (i j) -> f i j", j=NODES)
-            nc.vector.scalar_tensor_tensor(
-                out=slab_of[(b, c)][:, cols].rearrange("f (i j) -> f i j", j=NODES),
-                in0=product_of[(b, c, h)][:].rearrange("f (i j) -> f i j", j=NODES),
-                scalar=neg_b2_cols[:, c : c + 1],
-                in1=b2_plus_z,
-                op0=ALU.max,
-                op1=ALU.add,
+                for n in range(HALF // P):
+                    tile = TILES_PER_GROUP * group + (HALF // P) * h + n
+                    for t in range(PACK):
+                        nc.tensor.transpose(
+                            zt[:, t, P * n : P * (n + 1)], tail_rows[:, tile, t:K_PASS:PACK], ident_bf16[:]
+                        )
+            zt_of[(unit, h)] = zt
+
+        def add_z_in(unit, h):
+            if h == 0:
+                s_grouped = work.tile([P, GROUP, PACK], BF16, align_bytes=64, bufs=2)
+                s_grouped_of[unit] = s_grouped
+            rows = slice(HALF * h, HALF * (h + 1))
+            nc.vector.tensor_tensor(
+                out=s_grouped_of[unit][:, rows, :].rearrange("p (c i) t -> p c t i", i=4),
+                in0=m_of[unit][:, :, rows].rearrange("p t (c i) -> p c t i", i=4),
+                in1=zt_of[(unit, h)][:].rearrange("p t (c i) -> p c t i", i=4),
+                op=ALU.add,
             )
 
-        def regroup_partitions(b, c):
-            first_p = WORD_ROWS * (c % SLABS_PER_PASS)
-            for t in range(PACK):
-                nc.sync.dma_start(
-                    out=planes_of[b][first_p : first_p + WORD_ROWS, c // SLABS_PER_PASS, t, :],
-                    in_=slab_of[(b, c)][t:P:PACK, :],
-                )
-
-        def group_tile(tile, copy):
-            b, n = divmod(tile, TILES)
-            if tile // 2 not in s_grouped_of:
-                s_grouped = work.tile([P, 2, PASSES, P, PACK], BF16, align_bytes=64, bufs=4)
-                s_grouped_of[tile // 2] = s_grouped
-            for g in range(PASSES):
-                copy(
-                    out=s_grouped_of[tile // 2][:, tile % 2, g].rearrange("p (c i) t -> p c t i", i=4),
-                    in_=planes_of[b][:, g, :, P * n : P * (n + 1)].rearrange("p t (c i) -> p c t i", i=4),
-                )
-
-        def quantise_s(pair):
-            s_codes = work.tile([P, 2, PASSES, P], U32, align_bytes=64)
-            s_scales = work.tile([P, 2, PASSES, P], U8, align_bytes=64)
+        def quantise_s(unit):
+            s_codes = work.tile([P, GROUP], U32, align_bytes=64, bufs=4)
+            s_scales = work.tile([P, GROUP], U8, align_bytes=64, bufs=4)
             nc.vector.quantize_mx(
-                out=s_codes[:].rearrange("p n g q -> p (n g q)").bitcast(FP8X4),
-                scales=s_scales[:].rearrange("p n g q -> p (n g q)"),
-                in_=s_grouped_of[pair][:].rearrange("p n g q t -> p (n g q t)"),
+                out=s_codes[:].bitcast(FP8X4),
+                scales=s_scales[:],
+                in_=s_grouped_of[unit][:].rearrange("p q t -> p (q t)"),
             )
-            s_codes_of[pair] = (s_codes, s_scales)
+            s_codes_of[unit] = (s_codes, s_scales)
 
-        def second_matmul(tile):
-            s_codes, s_scales = s_codes_of[tile // 2]
-            y = psum.tile([P, ED], F32, tag="y", bufs=2)
-            for g in range(PASSES):
-                nc.tensor.matmul_mx(
-                    out=y[:],
-                    lhsT=s_codes[:, tile % 2, g, :].bitcast(FP8X4),
-                    lhsT_scale=s_scales[:, tile % 2, g, :],
-                    rhs=wo_words[:, g, :].bitcast(FP8X4),
-                    rhs_scale=wo_scales[:, g, :],
-                    start=(g == 0),
-                    stop=(g == PASSES - 1),
-                )
-            y_of[tile] = y
+        def second_matmul(pair):
+            y = psum.tile([P, 2, ED], F32, tag="y", bufs=1)
+            for n in range(2):
+                group, local = divmod(2 * pair + n, TILES_PER_GROUP)
+                cols = slice(P * local, P * (local + 1))
+                for g in range(PASSES):
+                    s_codes, s_scales = s_codes_of[PASSES * group + g]
+                    nc.tensor.matmul_mx(
+                        out=y[:, n, :],
+                        lhsT=s_codes[:, cols].bitcast(FP8X4),
+                        lhsT_scale=s_scales[:, cols],
+                        rhs=wo_words[:, g, :].bitcast(FP8X4),
+                        rhs_scale=wo_scales[:, g, :],
+                        start=(g == 0),
+                        stop=(g == PASSES - 1),
+                    )
+            y_of[pair] = y
 
         def add_bo(tile):
             z = work.tile([P, ED], F32, bufs=6)
-            z_sum = stats.tile([P, 1], F32)
+            z_sum = stats.tile([P, 1], F32, bufs=6)
             nc.vector.scalar_tensor_tensor(
-                out=z[:], in0=y_of[tile][:], scalar=0.0, in1=bo_rows[:], op0=ALU.add, op1=ALU.add, accum_out=z_sum[:]
+                out=z[:],
+                in0=y_of[tile // 2][:, tile % 2, :],
+                scalar=0.0,
+                in1=bo_rows[:],
+                op0=ALU.add,
+                op1=ALU.add,
+                accum_out=z_sum[:],
             )
             z_of[tile] = (z, z_sum)
 
@@ -318,9 +324,7 @@ def tile_edgeupdaterwrapper_v01_pb_t_kernel(
             nc.scalar.mul(out=neg_mean[:], in_=z_sum[:], mul=-1.0 / ED)
             unused = work.tile([P, ED], F32, bufs=2)
             sq_sum = stats.tile([P, 1], F32)
-            nc.scalar.activation(
-                out=unused[:], in_=z[:], func=ACT.Square, bias=neg_mean[:], accum_out=sq_sum[:]
-            )
+            nc.scalar.activation(out=unused[:], in_=z[:], func=ACT.Square, bias=neg_mean[:], accum_out=sq_sum[:])
             rstd = stats.tile([P, 1], F32, bufs=8)
             nc.scalar.activation(
                 out=rstd[:], in_=sq_sum[:], func=ACT.Abs_reciprocal_sqrt, scale=1.0 / ED, bias=eps_col[:]
@@ -328,7 +332,7 @@ def tile_edgeupdaterwrapper_v01_pb_t_kernel(
             stats_of[tile] = (neg_mean, rstd)
 
         def apply_gain(tile):
-            centred = work.tile([P, ED], F32)
+            centred = work.tile([P, ED], F32, bufs=4)
             nc.vector.scalar_tensor_tensor(
                 out=centred[:],
                 in0=z_of[tile][0][:],
@@ -358,41 +362,45 @@ def tile_edgeupdaterwrapper_v01_pb_t_kernel(
                 in_=result_of[pair][:],
             )
 
-        def grouped_by_scalar(tile):
-            return tile + SLAB_LEAD < ALL_TILES or tile % 2 == 1
-
-        for step in range(-PAIR_LEAD, ALL_TILES + 2 + LAG + 1):
-            done = step - 1 - LAG
-            if (step + LOAD_LEAD) % TILES == 0 and 2 <= (step + LOAD_LEAD) // TILES < BLOCKS:
-                load_hid((step + LOAD_LEAD) // TILES, range(PAIRS_PER_BLOCK))
-                load_p((step + LOAD_LEAD) // TILES)
-            half_step = step + PAIR_LEAD - LAG - 2
-            if half_step % 4 == 0 and 0 <= half_step // 4 < BLOCKS * HALVES:
-                quantise_hid(half_step // 4)
-            if 0 <= step < ALL_TILES and not grouped_by_scalar(step):
-                group_tile(step, nc.vector.tensor_copy)
-            if 0 <= done < ALL_TILES:
-                apply_gain(done)
-            if step % 2 == 0 and 0 <= step < ALL_TILES:
-                quantise_s(step // 2)
-            if 0 <= step + SLAB_LEAD + 1 < ALL_TILES:
-                first_matmul((step + SLAB_LEAD + 1) // TILES, (step + SLAB_LEAD + 1) % TILES)
-            if 0 <= step < ALL_TILES:
-                second_matmul(step)
-            if 0 <= step - 1 < ALL_TILES:
-                add_bo(step - 1)
-            if 0 <= step + SLAB_LEAD < ALL_TILES:
-                b, c = divmod(step + SLAB_LEAD, TILES)
-                for h in range(HALVES):
-                    make_s(b, c, h)
-                regroup_partitions(b, c)
-            if 0 <= done < ALL_TILES:
-                add_residual(done)
-                if done % 2 == 1:
-                    store_pair(done // 2)
-            if 0 <= step - 1 < ALL_TILES:
-                row_statistics(step - 1)
-            if 0 <= step + LAG + 1 < ALL_TILES and grouped_by_scalar(step + LAG + 1):
-                group_tile(step + LAG + 1, nc.scalar.copy)
-            if (step + PAIR_LEAD) % 2 == 0 and 0 <= (step + PAIR_LEAD) // 2 < ALL_PAIRS:
-                transpose_pair((step + PAIR_LEAD) // 2)
+        for step in range(-5, UNITS + 3):
+            ahead = step + 1
+            multiplied = step - 2
+            normed = step - 3
+            if 0 <= ahead < UNITS:
+                first_matmul(ahead)
+            if 0 <= multiplied < PAIRS:
+                second_matmul(multiplied)
+            if 0 <= normed < PAIRS:
+                row_statistics(2 * normed)
+                row_statistics(2 * normed + 1)
+            if 0 <= step + 4 < PAIRS:
+                group_hid(step + 4)
+            if 0 <= step < UNITS:
+                add_z_in(step, 0)
+            if 0 <= ahead < UNITS:
+                transpose_z_in(ahead, 0)
+            if 0 <= normed < PAIRS:
+                apply_gain(2 * normed)
+            if 0 <= step < UNITS:
+                add_z_in(step, 1)
+            if 0 <= ahead < UNITS:
+                transpose_z_in(ahead, 1)
+            if 0 <= step + 5 < PAIRS:
+                transpose_hid(step + 5)
+            if 0 <= ahead < UNITS:
+                for t in range(PACK):
+                    relu_out_of_psum(ahead, t)
+            if 0 <= normed < PAIRS:
+                apply_gain(2 * normed + 1)
+                add_residual(2 * normed)
+            if 0 <= multiplied < PAIRS:
+                add_bo(2 * multiplied)
+            if 0 <= normed < PAIRS:
+                add_residual(2 * normed + 1)
+                store_pair(normed)
+            if 0 <= multiplied < PAIRS:
+                add_bo(2 * multiplied + 1)
+            if 0 <= step < UNITS:
+                quantise_s(step)
+            if (step + 2) % 2 == 0 and 0 <= (step + 2) // 2 < GROUPS:
+                quantise_hid((step + 2) // 2)

@@ -66,8 +66,8 @@ def tile_edgeupdaterwrapper_v01_pb_t_kernel(
 
         hid_all = consts.tile([P, TILES, F], BF16)
         tail_rows = consts.tile([P, TILES, K_PASS], BF16)
-        residual_all = consts.tile([P, TILES, ED], F32)
         beta_rows = consts.tile([P, ED], BF16)
+        residual_all = consts.tile([P, TILES, ED], F32)
 
         def load_hid(first_tile, count):
             nc.sync.dma_start(
@@ -86,12 +86,13 @@ def tile_edgeupdaterwrapper_v01_pb_t_kernel(
                     out=tail_rows[NODES * half : NODES * (half + 1), tiles, 0:XJ_TAIL],
                     in_=x_down[0, :, XJ_HEAD:HD].unsqueeze(1).to_broadcast([NODES, count, XJ_TAIL]),
                 )
-            nc.gpsimd.tensor_tensor(
-                out=residual_all[:, tiles, :],
-                in0=tail_rows[:, tiles, XJ_TAIL:K_PASS],
-                in1=beta_rows[:].unsqueeze(1).to_broadcast([P, count, ED]),
-                op=ALU.add,
-            )
+            for first in range(first_tile, first_tile + count, 2):
+                nc.gpsimd.tensor_tensor(
+                    out=residual_all[:, first : first + 2, :],
+                    in0=tail_rows[:, first : first + 2, XJ_TAIL:K_PASS],
+                    in1=beta_rows[:].unsqueeze(1).to_broadcast([P, 2, ED]),
+                    op=ALU.add,
+                )
 
         w2_scales_raw = consts.tile([P, MD], U8, align_bytes=64)
         wo_scales = consts.tile([P, PASSES, ED], U8, align_bytes=64)
@@ -100,16 +101,18 @@ def tile_edgeupdaterwrapper_v01_pb_t_kernel(
         nc.vector.memset(head_rows[:], 0.0)
         nc.vector.memset(wo_scales[:].rearrange("p g n -> p (g n)").bitcast(I32), 0)
         load_hid(0, 2)
-        load_hid(2, 2)
         for quad in range(4):
             nc.sync.dma_start(
                 out=w2_scales_raw[32 * quad : 32 * quad + 4, :].bitcast(I32),
                 in_=W2_scales[0, 4 * quad : 4 * quad + 4, :].bitcast(I32),
             )
+        load_hid(2, 2)
         w2_words_raw = consts.tile([P, MD], U32, align_bytes=64)
-        nc.sync.dma_start(
-            out=w2_words_raw[:].bitcast(I32), in_=W2_words.rearrange("g p n t -> (g p) (n t)").bitcast(I32)
-        )
+        for g in range(PASSES):
+            nc.sync.dma_start(
+                out=w2_words_raw[:, K_PASS * g : K_PASS * (g + 1)].bitcast(I32),
+                in_=W2_words.rearrange("g p n t -> (g p) (n t)").bitcast(I32)[:, K_PASS * g : K_PASS * (g + 1)],
+            )
 
         b2_bf16 = consts.tile([P, SLABS], BF16)
         nc.scalar.dma_start(
@@ -132,27 +135,18 @@ def tile_edgeupdaterwrapper_v01_pb_t_kernel(
 
         selector = consts.tile([P, NODES, NODES], BF16)
 
-        def build_selector(group):
-            nodes = slice(I_PER_GROUP * group, I_PER_GROUP * (group + 1))
-            nc.gpsimd.tensor_scalar(
+        def build_selector(first_node, count):
+            nodes = slice(first_node, first_node + count)
+            nc.vector.tensor_copy(
                 out=selector[0:NODES, nodes, :],
-                in0=ident_bf16[0:NODES, nodes].unsqueeze(2).to_broadcast([NODES, I_PER_GROUP, NODES]),
-                scalar1=1.0,
-                scalar2=0.0,
-                op0=ALU.mult,
-                op1=ALU.add,
+                in_=ident_bf16[0:NODES, nodes].unsqueeze(2).to_broadcast([NODES, count, NODES]),
             )
-            nc.gpsimd.tensor_scalar(
+            nc.vector.tensor_copy(
                 out=selector[NODES:P, nodes, :],
-                in0=ident_bf16[NODES:P, NODES:P].unsqueeze(1).to_broadcast([NODES, I_PER_GROUP, NODES]),
-                scalar1=1.0,
-                scalar2=0.0,
-                op0=ALU.mult,
-                op1=ALU.add,
+                in_=ident_bf16[NODES:P, NODES:P].unsqueeze(1).to_broadcast([NODES, count, NODES]),
             )
 
-        build_selector(0)
-        build_selector(1)
+        build_selector(0, 2 * I_PER_GROUP)
         load_tail_rows(0, LOAD_TILES)
         load_hid(4, 4)
         for quad in range(4):
@@ -166,25 +160,26 @@ def tile_edgeupdaterwrapper_v01_pb_t_kernel(
         )
         for block in range(1, TILES // LOAD_TILES):
             load_hid(LOAD_TILES * block, 4)
-            build_selector(2 * block)
-            build_selector(2 * block + 1)
             load_tail_rows(LOAD_TILES * block, LOAD_TILES)
             load_hid(LOAD_TILES * block + 4, 4)
 
-        b2_cols = consts.tile([P, SLABS], F32)
-        nc.vector.tensor_copy(out=b2_cols[:], in_=b2_bf16[:])
-        head_slabs = consts.tile([P, PACK, P], BF16)
-        nc.vector.tensor_copy(out=head_slabs[:], in_=head_rows[:].rearrange("k (m t) -> k t m", t=PACK))
         w2_scales = consts.tile([P, MD], U8, align_bytes=64)
         nc.vector.tensor_copy(
             out=w2_scales[:].rearrange("p (g t m) -> p g m t", g=PASSES, t=PACK),
             in_=w2_scales_raw[:].rearrange("p (g m t) -> p g m t", g=PASSES, t=PACK),
         )
+        b2_cols = consts.tile([P, SLABS], F32)
+        nc.vector.tensor_copy(out=b2_cols[:], in_=b2_bf16[:])
+        head_slabs = consts.tile([P, PACK, P], BF16)
+        nc.vector.tensor_copy(out=head_slabs[:], in_=head_rows[:].rearrange("k (m t) -> k t m", t=PACK))
         w2_words = consts.tile([P, MD], U32, align_bytes=64)
-        nc.vector.tensor_copy(
-            out=w2_words[:].bitcast(I32).rearrange("p (g t m) -> p g t m", g=PASSES, t=PACK),
-            in_=w2_words_raw[:].bitcast(I32).rearrange("p (g m t) -> p g t m", g=PASSES, t=PACK),
-        )
+
+        def order_w2_words(g):
+            cols = slice(K_PASS * g, K_PASS * (g + 1))
+            nc.vector.tensor_copy(
+                out=w2_words[:, cols].bitcast(I32).rearrange("p (t m) -> p t m", t=PACK),
+                in_=w2_words_raw[:, cols].bitcast(I32).rearrange("p (m t) -> p t m", t=PACK),
+            )
 
         def transpose_hid(pair):
             word_t = psum.tile([P, 2, 2, P], F32, tag="word_t", bufs=1)
@@ -194,11 +189,11 @@ def tile_edgeupdaterwrapper_v01_pb_t_kernel(
                     nc.tensor.transpose(word_t[:, n, u, :], words[:, u : F // 2 : 2], ident_f32[:])
             word_t_of[pair] = word_t
 
-        def group_hid(pair):
+        def group_hid(pair, copy):
             if pair % 2 == 0:
                 hid_grouped = work.tile([P, 2, 2, P, PACK], BF16, align_bytes=64, bufs=2)
                 hid_grouped_of[pair // 2] = hid_grouped
-            nc.scalar.copy(
+            copy(
                 out=hid_grouped_of[pair // 2][:, pair % 2]
                 .rearrange("p n q t -> p (n q t)")
                 .bitcast(F32)
@@ -238,9 +233,22 @@ def tile_edgeupdaterwrapper_v01_pb_t_kernel(
                 m = work.tile([P, PACK, GROUP], F32)
                 m_of[unit] = m
             slab = PACK * (unit % PASSES) + t
-            nc.scalar.activation(
-                out=m_of[unit][:, t, :], in_=product_of[(unit, t)][:], func=ACT.Relu, bias=b2_cols[:, slab : slab + 1]
-            )
+            if unit == 0 and t >= PACK // 2:
+                nc.vector.tensor_scalar(
+                    out=m_of[unit][:, t, :],
+                    in0=product_of[(unit, t)][:],
+                    scalar1=b2_cols[:, slab : slab + 1],
+                    scalar2=0.0,
+                    op0=ALU.add,
+                    op1=ALU.max,
+                )
+            else:
+                nc.scalar.activation(
+                    out=m_of[unit][:, t, :],
+                    in_=product_of[(unit, t)][:],
+                    func=ACT.Relu,
+                    bias=b2_cols[:, slab : slab + 1],
+                )
 
         def transpose_z_in(unit, h):
             group, g = divmod(unit, PASSES)
@@ -347,13 +355,27 @@ def tile_edgeupdaterwrapper_v01_pb_t_kernel(
             if tile % 2 == 0:
                 result = work.tile([P, 2, ED], F32, bufs=4)
                 result_of[tile // 2] = result
-            nc.vector.scalar_tensor_tensor(
-                out=result_of[tile // 2][:, tile % 2, :],
+            if tile // 2 >= PAIRS - 2:
+                nc.vector.scalar_tensor_tensor(
+                    out=result_of[tile // 2][:, tile % 2, :],
+                    in0=centred_of[tile][:],
+                    scalar=stats_of[tile][1][:],
+                    in1=residual_all[:, tile, :],
+                    op0=ALU.mult,
+                    op1=ALU.add,
+                )
+                return
+            scaled = work.tile([P, ED], F32)
+            nc.gpsimd.tensor_scalar(
+                out=scaled[:],
                 in0=centred_of[tile][:],
-                scalar=stats_of[tile][1][:],
-                in1=residual_all[:, tile, :],
+                scalar1=stats_of[tile][1][:],
+                scalar2=0.0,
                 op0=ALU.mult,
                 op1=ALU.add,
+            )
+            nc.gpsimd.tensor_tensor(
+                out=result_of[tile // 2][:, tile % 2, :], in0=scaled[:], in1=residual_all[:, tile, :], op=ALU.add
             )
 
         def store_pair(pair):
@@ -374,7 +396,9 @@ def tile_edgeupdaterwrapper_v01_pb_t_kernel(
                 row_statistics(2 * normed)
                 row_statistics(2 * normed + 1)
             if 0 <= step + 4 < PAIRS:
-                group_hid(step + 4)
+                group_hid(step + 4, nc.vector.tensor_copy if step + 4 == 1 else nc.scalar.copy)
+            if step == -3:
+                order_w2_words(0)
             if 0 <= step < UNITS:
                 add_z_in(step, 0)
             if 0 <= ahead < UNITS:
@@ -404,3 +428,6 @@ def tile_edgeupdaterwrapper_v01_pb_t_kernel(
                 quantise_s(step)
             if (step + 2) % 2 == 0 and 0 <= (step + 2) // 2 < GROUPS:
                 quantise_hid((step + 2) // 2)
+            if step == -2:
+                order_w2_words(1)
+                build_selector(2 * I_PER_GROUP, NODES - 2 * I_PER_GROUP)

@@ -113,6 +113,16 @@ def tile_edgeupdaterwrapper_v01_pb_t_kernel(
                 out=w2_words_raw[:, K_PASS * g : K_PASS * (g + 1)].bitcast(I32),
                 in_=W2_words.rearrange("g p n t -> (g p) (n t)").bitcast(I32)[:, K_PASS * g : K_PASS * (g + 1)],
             )
+            load_hid(4 + 2 * g, 2)
+        w2_words = consts.tile([P, MD], U32, align_bytes=64)
+
+        def order_w2_words(g, copy):
+            cols = slice(K_PASS * g, K_PASS * (g + 1))
+            copy(
+                out=w2_words[:, cols].bitcast(I32).rearrange("p (t m) -> p t m", t=PACK),
+                in_=w2_words_raw[:, cols].bitcast(I32).rearrange("p (m t) -> p t m", t=PACK),
+            )
+
 
         b2_bf16 = consts.tile([P, SLABS], BF16)
         nc.scalar.dma_start(
@@ -135,20 +145,16 @@ def tile_edgeupdaterwrapper_v01_pb_t_kernel(
 
         selector = consts.tile([P, NODES, NODES], BF16)
 
-        def build_selector(first_node, count):
-            nodes = slice(first_node, first_node + count)
-            nc.vector.tensor_copy(
-                out=selector[0:NODES, nodes, :],
-                in_=ident_bf16[0:NODES, nodes].unsqueeze(2).to_broadcast([NODES, count, NODES]),
-            )
-            nc.vector.tensor_copy(
-                out=selector[NODES:P, nodes, :],
-                in_=ident_bf16[NODES:P, NODES:P].unsqueeze(1).to_broadcast([NODES, count, NODES]),
-            )
-
-        build_selector(0, 2 * I_PER_GROUP)
+        nc.vector.tensor_copy(
+            out=selector[0:NODES], in_=ident_bf16[0:NODES, 0:NODES].unsqueeze(2).to_broadcast([NODES, NODES, NODES])
+        )
+        early_nodes = 2 * I_PER_GROUP
+        nc.vector.tensor_copy(
+            out=selector[NODES:P, 0:early_nodes, :],
+            in_=ident_bf16[NODES:P, NODES:P].unsqueeze(1).to_broadcast([NODES, early_nodes, NODES]),
+        )
+        order_w2_words(1, nc.gpsimd.tensor_copy)
         load_tail_rows(0, LOAD_TILES)
-        load_hid(4, 4)
         for quad in range(4):
             nc.sync.dma_start(
                 out=wo_scales[32 * quad : 32 * quad + 4, :, :].bitcast(I32),
@@ -157,6 +163,14 @@ def tile_edgeupdaterwrapper_v01_pb_t_kernel(
         wo_words = consts.tile([P, PASSES, ED], U32, align_bytes=64)
         nc.sync.dma_start(
             out=wo_words[:].bitcast(I32), in_=Wo_words.rearrange("g p n t -> p g (n t)").bitcast(I32)
+        )
+        repeats = NODES // early_nodes - 1
+        nc.sync.dma_start(
+            out=selector[NODES:P, early_nodes:NODES, :].rearrange("k (r i) j -> k r (i j)", r=repeats),
+            in_=selector[NODES:P, 0:early_nodes, :]
+            .rearrange("k i j -> k (i j)")
+            .unsqueeze(1)
+            .to_broadcast([NODES, repeats, early_nodes * NODES]),
         )
         for block in range(1, TILES // LOAD_TILES):
             load_hid(LOAD_TILES * block, 4)
@@ -172,14 +186,12 @@ def tile_edgeupdaterwrapper_v01_pb_t_kernel(
         nc.vector.tensor_copy(out=b2_cols[:], in_=b2_bf16[:])
         head_slabs = consts.tile([P, PACK, P], BF16)
         nc.vector.tensor_copy(out=head_slabs[:], in_=head_rows[:].rearrange("k (m t) -> k t m", t=PACK))
-        w2_words = consts.tile([P, MD], U32, align_bytes=64)
+        gain_of = {}
 
-        def order_w2_words(g):
-            cols = slice(K_PASS * g, K_PASS * (g + 1))
-            nc.vector.tensor_copy(
-                out=w2_words[:, cols].bitcast(I32).rearrange("p (t m) -> p t m", t=PACK),
-                in_=w2_words_raw[:, cols].bitcast(I32).rearrange("p (m t) -> p t m", t=PACK),
-            )
+        def gain_into_psum():
+            gain_ps = psum.tile([P, ED], F32, tag="gain_ps", bufs=1)
+            nc.tensor.matmul(out=gain_ps[:], lhsT=ident_bf16[:], rhs=gain_rows[:], start=True, stop=True)
+            gain_of[0] = gain_ps
 
         def transpose_hid(pair):
             word_t = psum.tile([P, 2, 2, P], F32, tag="word_t", bufs=1)
@@ -211,12 +223,12 @@ def tile_edgeupdaterwrapper_v01_pb_t_kernel(
             )
             hid_codes_of[group] = (hid_codes, hid_scales)
 
-        def first_matmul(unit):
+        def first_matmul(unit, slabs):
             group, g = divmod(unit, PASSES)
             hid_codes, hid_scales = hid_codes_of[group]
-            for t in range(PACK):
+            for t in slabs:
                 cols = slice(P * (PACK * g + t), P * (PACK * g + t + 1))
-                product = psum.tile([P, GROUP], F32, tag="product", bufs=4)
+                product = psum.tile([P, GROUP], F32, tag="product", bufs=3)
                 nc.tensor.matmul_mx(
                     out=product[:],
                     lhsT=w2_words[:, cols].bitcast(FP8X4),
@@ -295,7 +307,10 @@ def tile_edgeupdaterwrapper_v01_pb_t_kernel(
             s_codes_of[unit] = (s_codes, s_scales)
 
         def second_matmul(pair):
-            y = psum.tile([P, 2, ED], F32, tag="y", bufs=1)
+            if pair < PAIRS - 1:
+                y = psum.tile([P, 2, ED], F32, tag="y", bufs=1)
+            else:
+                y = psum.tile([P, 2, ED], F32, tag="product", bufs=3)
             for n in range(2):
                 group, local = divmod(2 * pair + n, TILES_PER_GROUP)
                 cols = slice(P * local, P * (local + 1))
@@ -313,39 +328,49 @@ def tile_edgeupdaterwrapper_v01_pb_t_kernel(
             y_of[pair] = y
 
         def add_bo(tile):
-            z = work.tile([P, ED], F32, bufs=6)
-            z_sum = stats.tile([P, 1], F32, bufs=6)
+            if tile % 2 == 0:
+                z = work.tile([P, 2, ED], F32, bufs=4)
+                z_sum = stats.tile([P, 2], F32)
+                z_of[tile // 2] = (z, z_sum)
+            z, z_sum = z_of[tile // 2]
+            n = tile % 2
             nc.vector.scalar_tensor_tensor(
-                out=z[:],
-                in0=y_of[tile // 2][:, tile % 2, :],
+                out=z[:, n, :],
+                in0=y_of[tile // 2][:, n, :],
                 scalar=0.0,
                 in1=bo_rows[:],
                 op0=ALU.add,
                 op1=ALU.add,
-                accum_out=z_sum[:],
+                accum_out=z_sum[:, n : n + 1],
             )
-            z_of[tile] = (z, z_sum)
 
-        def row_statistics(tile):
-            z, z_sum = z_of[tile]
-            neg_mean = stats.tile([P, 1], F32, bufs=8)
+        def row_statistics(pair):
+            z, z_sum = z_of[pair]
+            neg_mean = stats.tile([P, 2], F32)
             nc.scalar.mul(out=neg_mean[:], in_=z_sum[:], mul=-1.0 / ED)
-            unused = work.tile([P, ED], F32, bufs=2)
-            sq_sum = stats.tile([P, 1], F32)
-            nc.scalar.activation(out=unused[:], in_=z[:], func=ACT.Square, bias=neg_mean[:], accum_out=sq_sum[:])
-            rstd = stats.tile([P, 1], F32, bufs=8)
+            sq_sum = stats.tile([P, 2], F32)
+            for n in range(2):
+                unused = work.tile([P, ED], F32, bufs=2)
+                nc.scalar.activation(
+                    out=unused[:],
+                    in_=z[:, n, :],
+                    func=ACT.Square,
+                    bias=neg_mean[:, n : n + 1],
+                    accum_out=sq_sum[:, n : n + 1],
+                )
+            rstd = stats.tile([P, 2], F32)
             nc.scalar.activation(
                 out=rstd[:], in_=sq_sum[:], func=ACT.Abs_reciprocal_sqrt, scale=1.0 / ED, bias=eps_col[:]
             )
-            stats_of[tile] = (neg_mean, rstd)
+            stats_of[pair] = (neg_mean, rstd)
 
         def apply_gain(tile):
             centred = work.tile([P, ED], F32, bufs=4)
             nc.vector.scalar_tensor_tensor(
                 out=centred[:],
-                in0=z_of[tile][0][:],
-                scalar=stats_of[tile][0][:],
-                in1=gain_rows[:],
+                in0=z_of[tile // 2][0][:, tile % 2, :],
+                scalar=stats_of[tile // 2][0][:, tile % 2 : tile % 2 + 1],
+                in1=gain_of[0][:],
                 op0=ALU.add,
                 op1=ALU.mult,
             )
@@ -359,7 +384,7 @@ def tile_edgeupdaterwrapper_v01_pb_t_kernel(
                 nc.vector.scalar_tensor_tensor(
                     out=result_of[tile // 2][:, tile % 2, :],
                     in0=centred_of[tile][:],
-                    scalar=stats_of[tile][1][:],
+                    scalar=stats_of[tile // 2][1][:, tile % 2 : tile % 2 + 1],
                     in1=residual_all[:, tile, :],
                     op0=ALU.mult,
                     op1=ALU.add,
@@ -369,7 +394,7 @@ def tile_edgeupdaterwrapper_v01_pb_t_kernel(
             nc.gpsimd.tensor_scalar(
                 out=scaled[:],
                 in0=centred_of[tile][:],
-                scalar1=stats_of[tile][1][:],
+                scalar1=stats_of[tile // 2][1][:, tile % 2 : tile % 2 + 1],
                 scalar2=0.0,
                 op0=ALU.mult,
                 op1=ALU.add,
@@ -384,27 +409,32 @@ def tile_edgeupdaterwrapper_v01_pb_t_kernel(
                 in_=result_of[pair][:],
             )
 
-        for step in range(-5, UNITS + 3):
+        for step in range(-5, UNITS + 2):
             ahead = step + 1
-            multiplied = step - 2
-            normed = step - 3
+            multiplied = [pair for pair in (step - 2, step - 1) if 0 <= pair < PAIRS and min(pair, PAIRS - 2) == step - 2]
+            normed = [pair for pair in (step - 3, step - 2) if 0 <= pair < PAIRS and min(pair, PAIRS - 2) == step - 3]
+            normed_tiles = [2 * pair + n for pair in normed for n in range(2)]
             if 0 <= ahead < UNITS:
-                first_matmul(ahead)
-            if 0 <= multiplied < PAIRS:
-                second_matmul(multiplied)
-            if 0 <= normed < PAIRS:
-                row_statistics(2 * normed)
-                row_statistics(2 * normed + 1)
+                first_matmul(ahead, range(0, PACK - 1))
+            for pair in normed:
+                row_statistics(pair)
+            if 0 <= ahead < UNITS:
+                relu_out_of_psum(ahead, 0)
+                relu_out_of_psum(ahead, 1)
+            for pair in multiplied:
+                second_matmul(pair)
+            if 0 <= ahead < UNITS:
+                first_matmul(ahead, range(PACK - 1, PACK))
+            if step == 0:
+                gain_into_psum()
             if 0 <= step + 4 < PAIRS:
                 group_hid(step + 4, nc.vector.tensor_copy if step + 4 == 1 else nc.scalar.copy)
             if step == -3:
-                order_w2_words(0)
+                order_w2_words(0, nc.vector.tensor_copy)
             if 0 <= step < UNITS:
                 add_z_in(step, 0)
             if 0 <= ahead < UNITS:
                 transpose_z_in(ahead, 0)
-            if 0 <= normed < PAIRS:
-                apply_gain(2 * normed)
             if 0 <= step < UNITS:
                 add_z_in(step, 1)
             if 0 <= ahead < UNITS:
@@ -412,22 +442,18 @@ def tile_edgeupdaterwrapper_v01_pb_t_kernel(
             if 0 <= step + 5 < PAIRS:
                 transpose_hid(step + 5)
             if 0 <= ahead < UNITS:
-                for t in range(PACK):
-                    relu_out_of_psum(ahead, t)
-            if 0 <= normed < PAIRS:
-                apply_gain(2 * normed + 1)
-                add_residual(2 * normed)
-            if 0 <= multiplied < PAIRS:
-                add_bo(2 * multiplied)
-            if 0 <= normed < PAIRS:
-                add_residual(2 * normed + 1)
-                store_pair(normed)
-            if 0 <= multiplied < PAIRS:
-                add_bo(2 * multiplied + 1)
+                relu_out_of_psum(ahead, 2)
+                relu_out_of_psum(ahead, 3)
+            for tile in normed_tiles:
+                apply_gain(tile)
+            for pair in normed:
+                add_residual(2 * pair)
+                add_residual(2 * pair + 1)
+                store_pair(pair)
+            for pair in multiplied:
+                add_bo(2 * pair)
+                add_bo(2 * pair + 1)
             if 0 <= step < UNITS:
                 quantise_s(step)
             if (step + 2) % 2 == 0 and 0 <= (step + 2) // 2 < GROUPS:
                 quantise_hid((step + 2) // 2)
-            if step == -2:
-                order_w2_words(1)
-                build_selector(2 * I_PER_GROUP, NODES - 2 * I_PER_GROUP)

@@ -285,26 +285,27 @@ def tile_edgeupdaterwrapper_v01_pb_t_kernel(
             zt_of[(unit, h)] = zt
 
         def add_z_in(unit, h):
-            if h == 0:
-                s_grouped = work.tile([P, GROUP, PACK], BF16, align_bytes=64, bufs=2)
-                s_grouped_of[unit] = s_grouped
+            group, g = divmod(unit, PASSES)
+            if g == 0 and h == 0:
+                s_grouped = work.tile([P, PASSES, GROUP, PACK], BF16, align_bytes=64, bufs=2)
+                s_grouped_of[group] = s_grouped
             rows = slice(HALF * h, HALF * (h + 1))
             nc.vector.tensor_tensor(
-                out=s_grouped_of[unit][:, rows, :].rearrange("p (c i) t -> p c t i", i=4),
+                out=s_grouped_of[group][:, g, rows, :].rearrange("p (c i) t -> p c t i", i=4),
                 in0=m_of[unit][:, :, rows].rearrange("p t (c i) -> p c t i", i=4),
                 in1=zt_of[(unit, h)][:].rearrange("p t (c i) -> p c t i", i=4),
                 op=ALU.add,
             )
 
-        def quantise_s(unit):
-            s_codes = work.tile([P, GROUP], U32, align_bytes=64, bufs=4)
-            s_scales = work.tile([P, GROUP], U8, align_bytes=64, bufs=4)
+        def quantise_s(group):
+            s_codes = work.tile([P, PASSES, GROUP], U32, align_bytes=64)
+            s_scales = work.tile([P, PASSES, GROUP], U8, align_bytes=64)
             nc.vector.quantize_mx(
-                out=s_codes[:].bitcast(FP8X4),
-                scales=s_scales[:],
-                in_=s_grouped_of[unit][:].rearrange("p q t -> p (q t)"),
+                out=s_codes[:].rearrange("p g q -> p (g q)").bitcast(FP8X4),
+                scales=s_scales[:].rearrange("p g q -> p (g q)"),
+                in_=s_grouped_of[group][:].rearrange("p g q t -> p (g q t)"),
             )
-            s_codes_of[unit] = (s_codes, s_scales)
+            s_codes_of[group] = (s_codes, s_scales)
 
         def second_matmul(pair):
             if pair < PAIRS - 1:
@@ -314,12 +315,12 @@ def tile_edgeupdaterwrapper_v01_pb_t_kernel(
             for n in range(2):
                 group, local = divmod(2 * pair + n, TILES_PER_GROUP)
                 cols = slice(P * local, P * (local + 1))
+                s_codes, s_scales = s_codes_of[group]
                 for g in range(PASSES):
-                    s_codes, s_scales = s_codes_of[PASSES * group + g]
                     nc.tensor.matmul_mx(
                         out=y[:, n, :],
-                        lhsT=s_codes[:, cols].bitcast(FP8X4),
-                        lhsT_scale=s_scales[:, cols],
+                        lhsT=s_codes[:, g, cols].bitcast(FP8X4),
+                        lhsT_scale=s_scales[:, g, cols],
                         rhs=wo_words[:, g, :].bitcast(FP8X4),
                         rhs_scale=wo_scales[:, g, :],
                         start=(g == 0),
@@ -453,7 +454,7 @@ def tile_edgeupdaterwrapper_v01_pb_t_kernel(
             for pair in multiplied:
                 add_bo(2 * pair)
                 add_bo(2 * pair + 1)
-            if 0 <= step < UNITS:
-                quantise_s(step)
+            if 0 <= step < UNITS and step % PASSES == PASSES - 1:
+                quantise_s(step // PASSES)
             if (step + 2) % 2 == 0 and 0 <= (step + 2) // 2 < GROUPS:
                 quantise_hid((step + 2) // 2)

@@ -34,6 +34,7 @@ XJ_TAIL = HD - XJ_HEAD
 I_PER_GROUP = GROUP // NODES
 I_PER_HALF = HALF // NODES
 LOAD_TILES = 8
+EARLY_RESIDUALS = 8
 EPS = 1e-5
 
 FLOPS = 2 * ROWS * F * MD + 2 * ROWS * MD * ED
@@ -75,6 +76,14 @@ def tile_edgeupdaterwrapper_v01_pb_t_kernel(
                 in_=hid_rows_all[P * first_tile : P * (first_tile + count), :].rearrange("(n q) k -> q n k", q=P),
             )
 
+        def make_residual(pair):
+            nc.gpsimd.tensor_tensor(
+                out=residual_all[:, 2 * pair : 2 * pair + 2, :],
+                in0=tail_rows[:, 2 * pair : 2 * pair + 2, XJ_TAIL:K_PASS],
+                in1=beta_rows[:].unsqueeze(1).to_broadcast([P, 2, ED]),
+                op=ALU.add,
+            )
+
         def load_tail_rows(first_tile, count):
             tiles = slice(first_tile, first_tile + count)
             nc.sync.dma_start(
@@ -86,13 +95,9 @@ def tile_edgeupdaterwrapper_v01_pb_t_kernel(
                     out=tail_rows[NODES * half : NODES * (half + 1), tiles, 0:XJ_TAIL],
                     in_=x_down[0, :, XJ_HEAD:HD].unsqueeze(1).to_broadcast([NODES, count, XJ_TAIL]),
                 )
-            for first in range(first_tile, first_tile + count, 2):
-                nc.gpsimd.tensor_tensor(
-                    out=residual_all[:, first : first + 2, :],
-                    in0=tail_rows[:, first : first + 2, XJ_TAIL:K_PASS],
-                    in1=beta_rows[:].unsqueeze(1).to_broadcast([P, 2, ED]),
-                    op=ALU.add,
-                )
+            for pair in range(first_tile // 2, (first_tile + count) // 2):
+                if pair < EARLY_RESIDUALS:
+                    make_residual(pair)
 
         w2_scales_raw = consts.tile([P, MD], U8, align_bytes=64)
         wo_scales = consts.tile([P, PASSES, ED], U8, align_bytes=64)
@@ -366,7 +371,7 @@ def tile_edgeupdaterwrapper_v01_pb_t_kernel(
             stats_of[pair] = (neg_mean, rstd)
 
         def apply_gain(tile):
-            centred = work.tile([P, ED], F32, bufs=4)
+            centred = work.tile([P, ED], F32, bufs=8)
             nc.vector.scalar_tensor_tensor(
                 out=centred[:],
                 in0=z_of[tile // 2][0][:, tile % 2, :],
@@ -451,6 +456,8 @@ def tile_edgeupdaterwrapper_v01_pb_t_kernel(
                 add_residual(2 * pair)
                 add_residual(2 * pair + 1)
                 store_pair(pair)
+                if pair + EARLY_RESIDUALS < PAIRS:
+                    make_residual(pair + EARLY_RESIDUALS)
             for pair in multiplied:
                 add_bo(2 * pair)
                 add_bo(2 * pair + 1)

import concourse.mybir as mybir
from concourse.masks import make_identity

F32 = mybir.dt.float32
BF16 = mybir.dt.bfloat16
I32 = mybir.dt.int32
U32 = mybir.dt.uint32
U8 = mybir.dt.uint8
FP8X4 = mybir.dt.float8_e4m3fn_x4
ALU = mybir.AluOpType
ACT = mybir.ActivationFunctionType

P = 128
PACK = 4
NODES = 64
HD = 384
ED = 256
F = 512
MD = HD + HD + ED
K_PASS = P * PACK
PASSES = MD // K_PASS
SLABS = PASSES * PACK
ROWS = NODES * NODES
GROUP = 512
GROUPS = ROWS // GROUP
HALF = GROUP // 2
TILES = ROWS // P
PAIRS = TILES // 2
TILES_PER_GROUP = GROUP // P
UNITS = GROUPS * PASSES
XI_PARTS = HD // PACK
XJ_HEAD = K_PASS - HD
XJ_TAIL = HD - XJ_HEAD
I_PER_GROUP = GROUP // NODES
I_PER_HALF = HALF // NODES
LOAD_TILES = 8
EARLY_RESIDUALS = 8
EPS = 1e-5

FLOPS = 2 * ROWS * F * MD + 2 * ROWS * MD * ED


def tile_edgeupdaterwrapper_v01_pb_t_kernel(
    tc, hid, x_down, p_ln, W2_words, W2_scales, b2, Wo_words, Wo_scales, bo, ln_out_g, ln_out_b, out
):
    nc = tc.nc
    hid_rows_all = hid.rearrange("b i j k -> (b i j) k")
    p_rows_all = p_ln.rearrange("b i j d -> (b i j) d")
    out_rows_all = out.rearrange("b i j d -> (b i j) d")

    with tc.tile_pool(name="consts", bufs=1) as consts, tc.tile_pool(name="work", bufs=3) as work, tc.tile_pool(
        name="stats", bufs=4
    ) as stats, tc.psum_pool(name="psum", bufs=2) as psum, tc.manual_schedule():
        hid_grouped_of = {}
        hid_codes_of = {}
        word_t_of = {}
        product_of = {}
        m_of = {}
        zt_of = {}
        s_grouped_of = {}
        s_codes_of = {}
        y_of = {}
        z_of = {}
        stats_of = {}
        centred_of = {}
        result_of = {}

        hid_all = consts.tile([P, TILES, F], BF16)
        tail_rows = consts.tile([P, TILES, K_PASS], BF16)
        beta_rows = consts.tile([P, ED], BF16)
        residual_all = consts.tile([P, TILES, ED], F32)

        def load_hid(first_tile, count):
            nc.sync.dma_start(
                out=hid_all[:, first_tile : first_tile + count, :],
                in_=hid_rows_all[P * first_tile : P * (first_tile + count), :].rearrange("(n q) k -> q n k", q=P),
            )

        def make_residual(pair):
            nc.gpsimd.tensor_tensor(
                out=residual_all[:, 2 * pair : 2 * pair + 2, :],
                in0=tail_rows[:, 2 * pair : 2 * pair + 2, XJ_TAIL:K_PASS],
                in1=beta_rows[:].unsqueeze(1).to_broadcast([P, 2, ED]),
                op=ALU.add,
            )

        def load_tail_rows(first_tile, count):
            tiles = slice(first_tile, first_tile + count)
            nc.sync.dma_start(
                out=tail_rows[:, tiles, XJ_TAIL:K_PASS],
                in_=p_rows_all[P * first_tile : P * (first_tile + count), :].rearrange("(n q) d -> q n d", q=P),
            )
            for half in range(P // NODES):
                nc.sync.dma_start(
                    out=tail_rows[NODES * half : NODES * (half + 1), tiles, 0:XJ_TAIL],
                    in_=x_down[0, :, XJ_HEAD:HD].unsqueeze(1).to_broadcast([NODES, count, XJ_TAIL]),
                )
            for pair in range(first_tile // 2, (first_tile + count) // 2):
                if pair < EARLY_RESIDUALS:
                    make_residual(pair)

        w2_scales_raw = consts.tile([P, MD], U8, align_bytes=64)
        wo_scales = consts.tile([P, PASSES, ED], U8, align_bytes=64)
        head_rows = consts.tile([P, K_PASS], BF16)
        nc.vector.memset(w2_scales_raw[:].bitcast(I32), 0)
        nc.vector.memset(head_rows[:], 0.0)
        nc.vector.memset(wo_scales[:].rearrange("p g n -> p (g n)").bitcast(I32), 0)
        load_hid(0, 2)
        for quad in range(4):
            nc.sync.dma_start(
                out=w2_scales_raw[32 * quad : 32 * quad + 4, :].bitcast(I32),
                in_=W2_scales[0, 4 * quad : 4 * quad + 4, :].bitcast(I32),
            )
        load_hid(2, 2)
        w2_words_raw = consts.tile([P, MD], U32, align_bytes=64)
        for g in range(PASSES):
            nc.sync.dma_start(
                out=w2_words_raw[:, K_PASS * g : K_PASS * (g + 1)].bitcast(I32),
                in_=W2_words.rearrange("g p n t -> (g p) (n t)").bitcast(I32)[:, K_PASS * g : K_PASS * (g + 1)],
            )
            load_hid(4 + 2 * g, 2)
        w2_words = consts.tile([P, MD], U32, align_bytes=64)

        def order_w2_words(g, copy):
            cols = slice(K_PASS * g, K_PASS * (g + 1))
            copy(
                out=w2_words[:, cols].bitcast(I32).rearrange("p (t m) -> p t m", t=PACK),
                in_=w2_words_raw[:, cols].bitcast(I32).rearrange("p (m t) -> p t m", t=PACK),
            )


        b2_bf16 = consts.tile([P, SLABS], BF16)
        nc.scalar.dma_start(
            out=b2_bf16[:].rearrange("p (g t) -> p g t", t=PACK), in_=b2.rearrange("(g p t) -> p g t", g=PASSES, t=PACK)
        )
        nc.scalar.dma_start(out=head_rows[0:NODES, 0:HD], in_=x_down[0, :, :])
        nc.scalar.dma_start(out=head_rows[NODES:P, HD:K_PASS], in_=x_down[0, :, 0:XJ_HEAD])
        nc.scalar.dma_start(out=beta_rows[:], in_=ln_out_b.partition_broadcast(P))
        bo_rows = consts.tile([P, ED], BF16)
        nc.scalar.dma_start(out=bo_rows[:], in_=bo.partition_broadcast(P))
        gain_rows = consts.tile([P, ED], BF16)
        nc.scalar.dma_start(out=gain_rows[:], in_=ln_out_g.partition_broadcast(P))
        eps_col = consts.tile([P, 1], F32)
        nc.vector.memset(eps_col[:], EPS)

        ident_f32 = consts.tile([P, P], F32)
        make_identity(nc, ident_f32[:])
        ident_bf16 = consts.tile([P, P], BF16)
        make_identity(nc, ident_bf16[:])

        selector = consts.tile([P, NODES, NODES], BF16)

        nc.vector.tensor_copy(
            out=selector[0:NODES], in_=ident_bf16[0:NODES, 0:NODES].unsqueeze(2).to_broadcast([NODES, NODES, NODES])
        )
        early_nodes = 2 * I_PER_GROUP
        nc.vector.tensor_copy(
            out=selector[NODES:P, 0:early_nodes, :],
            in_=ident_bf16[NODES:P, NODES:P].unsqueeze(1).to_broadcast([NODES, early_nodes, NODES]),
        )
        order_w2_words(1, nc.gpsimd.tensor_copy)
        load_tail_rows(0, LOAD_TILES)
        for quad in range(4):
            nc.sync.dma_start(
                out=wo_scales[32 * quad : 32 * quad + 4, :, :].bitcast(I32),
                in_=Wo_scales[:, 4 * quad : 4 * quad + 4, :].rearrange("g r n -> r g n").bitcast(I32),
            )
        wo_words = consts.tile([P, PASSES, ED], U32, align_bytes=64)
        nc.sync.dma_start(
            out=wo_words[:].bitcast(I32), in_=Wo_words.rearrange("g p n t -> p g (n t)").bitcast(I32)
        )
        repeats = NODES // early_nodes - 1
        nc.sync.dma_start(
            out=selector[NODES:P, early_nodes:NODES, :].rearrange("k (r i) j -> k r (i j)", r=repeats),
            in_=selector[NODES:P, 0:early_nodes, :]
            .rearrange("k i j -> k (i j)")
            .unsqueeze(1)
            .to_broadcast([NODES, repeats, early_nodes * NODES]),
        )
        for block in range(1, TILES // LOAD_TILES):
            load_hid(LOAD_TILES * block, 4)
            load_tail_rows(LOAD_TILES * block, LOAD_TILES)
            load_hid(LOAD_TILES * block + 4, 4)

        w2_scales = consts.tile([P, MD], U8, align_bytes=64)
        nc.vector.tensor_copy(
            out=w2_scales[:].rearrange("p (g t m) -> p g m t", g=PASSES, t=PACK),
            in_=w2_scales_raw[:].rearrange("p (g m t) -> p g m t", g=PASSES, t=PACK),
        )
        b2_cols = consts.tile([P, SLABS], F32)
        nc.vector.tensor_copy(out=b2_cols[:], in_=b2_bf16[:])
        head_slabs = consts.tile([P, PACK, P], BF16)
        nc.vector.tensor_copy(out=head_slabs[:], in_=head_rows[:].rearrange("k (m t) -> k t m", t=PACK))
        gain_of = {}

        def gain_into_psum():
            gain_ps = psum.tile([P, ED], F32, tag="gain_ps", bufs=1)
            nc.tensor.matmul(out=gain_ps[:], lhsT=ident_bf16[:], rhs=gain_rows[:], start=True, stop=True)
            gain_of[0] = gain_ps

        def transpose_hid(pair):
            word_t = psum.tile([P, 2, 2, P], F32, tag="word_t", bufs=1)
            for n in range(2):
                words = hid_all[:, 2 * pair + n, :].bitcast(F32)
                for u in range(2):
                    nc.tensor.transpose(word_t[:, n, u, :], words[:, u : F // 2 : 2], ident_f32[:])
            word_t_of[pair] = word_t

        def group_hid(pair, copy):
            if pair % 2 == 0:
                hid_grouped = work.tile([P, 2, 2, P, PACK], BF16, align_bytes=64, bufs=2)
                hid_grouped_of[pair // 2] = hid_grouped
            copy(
                out=hid_grouped_of[pair // 2][:, pair % 2]
                .rearrange("p n q t -> p (n q t)")
                .bitcast(F32)
                .rearrange("p (n q u) -> p n q u", n=2, u=2),
                in_=word_t_of[pair][:].rearrange("p n u q -> p n q u"),
            )

        def quantise_hid(group):
            hid_codes = work.tile([P, GROUP], U32, align_bytes=64)
            hid_scales = work.tile([P, GROUP], U8, align_bytes=64)
            nc.vector.quantize_mx(
                out=hid_codes[:].bitcast(FP8X4),
                scales=hid_scales[:],
                in_=hid_grouped_of[group][:].rearrange("p m n q t -> p (m n q t)"),
            )
            hid_codes_of[group] = (hid_codes, hid_scales)

        def first_matmul(unit, slabs):
            group, g = divmod(unit, PASSES)
            hid_codes, hid_scales = hid_codes_of[group]
            for t in slabs:
                cols = slice(P * (PACK * g + t), P * (PACK * g + t + 1))
                product = psum.tile([P, GROUP], F32, tag="product", bufs=3)
                nc.tensor.matmul_mx(
                    out=product[:],
                    lhsT=w2_words[:, cols].bitcast(FP8X4),
                    lhsT_scale=w2_scales[:, cols],
                    rhs=hid_codes[:].bitcast(FP8X4),
                    rhs_scale=hid_scales[:],
                    start=True,
                    stop=True,
                )
                product_of[(unit, t)] = product

        def relu_out_of_psum(unit, t):
            if t == 0:
                m = work.tile([P, PACK, GROUP], F32)
                m_of[unit] = m
            slab = PACK * (unit % PASSES) + t
            if unit == 0 and t >= PACK // 2:
                nc.vector.tensor_scalar(
                    out=m_of[unit][:, t, :],
                    in0=product_of[(unit, t)][:],
                    scalar1=b2_cols[:, slab : slab + 1],
                    scalar2=0.0,
                    op0=ALU.add,
                    op1=ALU.max,
                )
            else:
                nc.scalar.activation(
                    out=m_of[unit][:, t, :],
                    in_=product_of[(unit, t)][:],
                    func=ACT.Relu,
                    bias=b2_cols[:, slab : slab + 1],
                )

        def transpose_z_in(unit, h):
            group, g = divmod(unit, PASSES)
            zt = psum.tile([P, PACK, HALF], BF16, tag="zt", bufs=2)
            if g == 0:
                first_i = I_PER_GROUP * group + I_PER_HALF * h
                for t in range(PACK):
                    nc.tensor.matmul(
                        out=zt[:, t, :],
                        lhsT=head_slabs[:, t, :],
                        rhs=selector[:, first_i : first_i + I_PER_HALF, :].rearrange("k i j -> k (i j)"),
                        start=True,
                        stop=True,
                    )
            else:
                for n in range(HALF // P):
                    tile = TILES_PER_GROUP * group + (HALF // P) * h + n
                    for t in range(PACK):
                        nc.tensor.transpose(
                            zt[:, t, P * n : P * (n + 1)], tail_rows[:, tile, t:K_PASS:PACK], ident_bf16[:]
                        )
            zt_of[(unit, h)] = zt

        def add_z_in(unit, h):
            group, g = divmod(unit, PASSES)
            if g == 0 and h == 0:
                s_grouped = work.tile([P, PASSES, GROUP, PACK], BF16, align_bytes=64, bufs=2)
                s_grouped_of[group] = s_grouped
            rows = slice(HALF * h, HALF * (h + 1))
            nc.vector.tensor_tensor(
                out=s_grouped_of[group][:, g, rows, :].rearrange("p (c i) t -> p c t i", i=4),
                in0=m_of[unit][:, :, rows].rearrange("p t (c i) -> p c t i", i=4),
                in1=zt_of[(unit, h)][:].rearrange("p t (c i) -> p c t i", i=4),
                op=ALU.add,
            )

        def quantise_s(group):
            s_codes = work.tile([P, PASSES, GROUP], U32, align_bytes=64)
            s_scales = work.tile([P, PASSES, GROUP], U8, align_bytes=64)
            nc.vector.quantize_mx(
                out=s_codes[:].rearrange("p g q -> p (g q)").bitcast(FP8X4),
                scales=s_scales[:].rearrange("p g q -> p (g q)"),
                in_=s_grouped_of[group][:].rearrange("p g q t -> p (g q t)"),
            )
            s_codes_of[group] = (s_codes, s_scales)

        def second_matmul(pair):
            if pair < PAIRS - 1:
                y = psum.tile([P, 2, ED], F32, tag="y", bufs=1)
            else:
                y = psum.tile([P, 2, ED], F32, tag="product", bufs=3)
            for n in range(2):
                group, local = divmod(2 * pair + n, TILES_PER_GROUP)
                cols = slice(P * local, P * (local + 1))
                s_codes, s_scales = s_codes_of[group]
                for g in range(PASSES):
                    nc.tensor.matmul_mx(
                        out=y[:, n, :],
                        lhsT=s_codes[:, g, cols].bitcast(FP8X4),
                        lhsT_scale=s_scales[:, g, cols],
                        rhs=wo_words[:, g, :].bitcast(FP8X4),
                        rhs_scale=wo_scales[:, g, :],
                        start=(g == 0),
                        stop=(g == PASSES - 1),
                    )
            y_of[pair] = y

        def add_bo(tile):
            if tile % 2 == 0:
                z = work.tile([P, 2, ED], F32, bufs=4)
                z_sum = stats.tile([P, 2], F32)
                z_of[tile // 2] = (z, z_sum)
            z, z_sum = z_of[tile // 2]
            n = tile % 2
            nc.vector.scalar_tensor_tensor(
                out=z[:, n, :],
                in0=y_of[tile // 2][:, n, :],
                scalar=0.0,
                in1=bo_rows[:],
                op0=ALU.add,
                op1=ALU.add,
                accum_out=z_sum[:, n : n + 1],
            )

        def row_statistics(pair):
            z, z_sum = z_of[pair]
            neg_mean = stats.tile([P, 2], F32)
            nc.scalar.mul(out=neg_mean[:], in_=z_sum[:], mul=-1.0 / ED)
            sq_sum = stats.tile([P, 2], F32)
            for n in range(2):
                unused = work.tile([P, ED], F32, bufs=2)
                nc.scalar.activation(
                    out=unused[:],
                    in_=z[:, n, :],
                    func=ACT.Square,
                    bias=neg_mean[:, n : n + 1],
                    accum_out=sq_sum[:, n : n + 1],
                )
            rstd = stats.tile([P, 2], F32)
            nc.scalar.activation(
                out=rstd[:], in_=sq_sum[:], func=ACT.Abs_reciprocal_sqrt, scale=1.0 / ED, bias=eps_col[:]
            )
            stats_of[pair] = (neg_mean, rstd)

        def apply_gain(tile):
            centred = work.tile([P, ED], F32, bufs=8)
            nc.vector.scalar_tensor_tensor(
                out=centred[:],
                in0=z_of[tile // 2][0][:, tile % 2, :],
                scalar=stats_of[tile // 2][0][:, tile % 2 : tile % 2 + 1],
                in1=gain_of[0][:],
                op0=ALU.add,
                op1=ALU.mult,
            )
            centred_of[tile] = centred

        def add_residual(tile):
            if tile % 2 == 0:
                result = work.tile([P, 2, ED], F32, bufs=4)
                result_of[tile // 2] = result
            if tile // 2 >= PAIRS - 2:
                nc.vector.scalar_tensor_tensor(
                    out=result_of[tile // 2][:, tile % 2, :],
                    in0=centred_of[tile][:],
                    scalar=stats_of[tile // 2][1][:, tile % 2 : tile % 2 + 1],
                    in1=residual_all[:, tile, :],
                    op0=ALU.mult,
                    op1=ALU.add,
                )
                return
            scaled = work.tile([P, ED], F32)
            nc.gpsimd.tensor_scalar(
                out=scaled[:],
                in0=centred_of[tile][:],
                scalar1=stats_of[tile // 2][1][:, tile % 2 : tile % 2 + 1],
                scalar2=0.0,
                op0=ALU.mult,
                op1=ALU.add,
            )
            nc.gpsimd.tensor_tensor(
                out=result_of[tile // 2][:, tile % 2, :], in0=scaled[:], in1=residual_all[:, tile, :], op=ALU.add
            )

        def store_pair(pair):
            nc.sync.dma_start(
                out=out_rows_all[2 * P * pair : 2 * P * (pair + 1), :].rearrange("(n q) d -> q n d", q=P),
                in_=result_of[pair][:],
            )

        for step in range(-5, UNITS + 2):
            ahead = step + 1
            multiplied = [pair for pair in (step - 2, step - 1) if 0 <= pair < PAIRS and min(pair, PAIRS - 2) == step - 2]
            normed = [pair for pair in (step - 3, step - 2) if 0 <= pair < PAIRS and min(pair, PAIRS - 2) == step - 3]
            normed_tiles = [2 * pair + n for pair in normed for n in range(2)]
            if 0 <= ahead < UNITS:
                first_matmul(ahead, range(0, PACK - 1))
            for pair in normed:
                row_statistics(pair)
            if 0 <= ahead < UNITS:
                relu_out_of_psum(ahead, 0)
                relu_out_of_psum(ahead, 1)
            for pair in multiplied:
                second_matmul(pair)
            if 0 <= ahead < UNITS:
                first_matmul(ahead, range(PACK - 1, PACK))
            if step == 0:
                gain_into_psum()
            if 0 <= step + 4 < PAIRS:
                group_hid(step + 4, nc.vector.tensor_copy if step + 4 == 1 else nc.scalar.copy)
            if step == -3:
                order_w2_words(0, nc.vector.tensor_copy)
            if 0 <= step < UNITS:
                add_z_in(step, 0)
            if 0 <= ahead < UNITS:
                transpose_z_in(ahead, 0)
            if 0 <= step < UNITS:
                add_z_in(step, 1)
            if 0 <= ahead < UNITS:
                transpose_z_in(ahead, 1)
            if 0 <= step + 5 < PAIRS:
                transpose_hid(step + 5)
            if 0 <= ahead < UNITS:
                relu_out_of_psum(ahead, 2)
                relu_out_of_psum(ahead, 3)
            for tile in normed_tiles:
                apply_gain(tile)
            for pair in normed:
                add_residual(2 * pair)
                add_residual(2 * pair + 1)
                store_pair(pair)
                if pair + EARLY_RESIDUALS < PAIRS:
                    make_residual(pair + EARLY_RESIDUALS)
            for pair in multiplied:
                add_bo(2 * pair)
                add_bo(2 * pair + 1)
            if 0 <= step < UNITS and step % PASSES == PASSES - 1:
                quantise_s(step // PASSES)
            if (step + 2) % 2 == 0 and 0 <= (step + 2) // 2 < GROUPS:
                quantise_hid((step + 2) // 2)
